import numpy as np
import ml_dtypes


def mxq(x, axis, fmt="e4m3"):
    dtype, down = {"e4m3": (ml_dtypes.float8_e4m3fn, 7), "e5m2": (ml_dtypes.float8_e5m2, 14)}[fmt]
    v = np.moveaxis(np.asarray(x, np.float32).astype(ml_dtypes.bfloat16).astype(np.float64), axis, -1)
    blocks = v.reshape(v.shape[:-1] + (-1, 32))
    amax = np.abs(blocks).max(-1, keepdims=True)
    byte = np.maximum(np.where(amax > 0, np.frexp(amax)[1] - 1 + 127, 0) - down, 1)
    scale = np.exp2(byte - 127.0)
    codes = (blocks / scale).astype(np.float32).astype(dtype).astype(np.float64)
    return np.moveaxis((codes * scale).reshape(v.shape), -1, axis)


WIDE = False


def mx_kscale(k):
    if not WIDE:
        return np.ones(k)
    levels = np.array([10, -10, 5, -5, 0])
    a = np.random.permutation(np.resize(levels, k // 512 * 4)).reshape(k // 512, 4)
    idx = np.arange(k)
    return np.exp2(a[idx // 512, idx % 128 // 32])


BF16 = ml_dtypes.bfloat16


def bf(x):
    return np.asarray(x, np.float32).astype(BF16)


def f64(x):
    return np.asarray(x).astype(np.float64)


B, D, L, H = 8192, 512, 128, 1024


def sigmoid(v):
    return 1.0 / (1.0 + np.exp(-v))


def setup_inputs():
    t = mx_kscale(H)
    return {
        "z": bf(np.random.standard_normal((B, L)) * 1.7),
        "x": bf(np.random.random((B, D)) < 0.5),
        "Wd1": bf(np.random.standard_normal((L, H)) * 0.6 / np.sqrt(L) * t),
        "bd1": bf(np.random.standard_normal(H) * 0.5 * t),
        "Wd2": bf(np.random.standard_normal((H, D)) * 2.8 / np.sqrt(H) / t[:, None]),
        "bd2": bf(np.random.standard_normal(D) * 0.5),
    }


def reference(z, x, Wd1, bd1, Wd2, bd2):
    x = f64(x)
    hd = np.maximum(f64(z) @ f64(Wd1) + f64(bd1), 0.0)
    theta = sigmoid((mxq(hd, 1, "e4m3") @ mxq(f64(Wd2), 0, "e4m3")) + f64(bd2))
    return np.sum(x * np.log(theta) + (1.0 - x) * np.log1p(-theta), axis=-1)

@@ -1,0 +1,251 @@
+from contextlib import ExitStack
+
+import concourse.mybir as mybir
+from concourse.masks import make_identity
+
+F32 = mybir.dt.float32
+BF16 = mybir.dt.bfloat16
+U32 = mybir.dt.uint32
+U8 = mybir.dt.uint8
+FP8X4 = mybir.dt.float8_e4m3fn_x4
+ALU = mybir.AluOpType
+ACT = mybir.ActivationFunctionType
+
+B, D, L, H = 8192, 512, 128, 1024
+P = 128
+PACK = 4
+PASSES = H // (P * PACK)
+TILES = B // P
+Q = 4
+MACROS = TILES // Q
+W = Q * P
+PLANES = PASSES * PACK
+FLOPS = 2 * B * (L * H + H * D)
+
+GROUPS = [6, 6, 4]
+DLAG = 5
+KV = [2] * 16
+JPI = [0, 1, 1, 2, 2, 2, 2, 2, 2, 2, 2, 2, 2]
+XLAG = 1
+NV = 7
+NE = 8
+NX = 3
+ZCH = [1, 3, 4, 8]
+
+
+def tile_vae_pb_t_kernel(tc, z, x, Wd1, bd1, Wd2, bd2, out):
+    nc = tc.nc
+    z_v = z.rearrange("(p i) l -> p i l", i=TILES)
+    x_v = x.rearrange("(p i) j -> p i j", i=TILES)
+    out_v = out.rearrange("(p i) -> p i", i=TILES)
+    with ExitStack() as ctx:
+        const = ctx.enter_context(tc.tile_pool(name="const", bufs=1))
+        work = ctx.enter_context(tc.tile_pool(name="work", bufs=2))
+        psum1 = ctx.enter_context(tc.psum_pool(name="psum1", bufs=3))
+        psum2 = ctx.enter_context(tc.psum_pool(name="psum2", bufs=4))
+        psumt = ctx.enter_context(tc.psum_pool(name="psumt", bufs=1))
+        ctx.enter_context(tc.manual_schedule())
+
+        zch = []
+        m0 = 0
+        for k, n in enumerate(ZCH):
+            zt = const.tile([P, n * Q, L], BF16, name="zc%d" % k)
+            zch.append((m0, n, zt))
+            m0 += n
+        def load_z(k):
+            m0, n, zt = zch[k]
+            nc.sync.dma_start(out=zt[:], in_=z_v[:, m0 * Q:(m0 + n) * Q, :])
+        w1_raw = const.tile([P, H], BF16, name="w1_raw")
+        b1_raw = const.tile([P, PASSES, PACK], BF16, name="b1_raw")
+        w2_raw = const.tile([P, PASSES, PACK, D], BF16, name="w2_raw")
+        b2b = const.tile([P, D], BF16, name="b2b")
+        load_z(0)
+        nc.sync.dma_start(out=w1_raw[:], in_=Wd1)
+        nc.sync.dma_start(out=b1_raw[:], in_=bd1.rearrange("(c p t) -> p c t", c=PASSES, t=PACK))
+        load_z(1)
+        w2_v = Wd2.rearrange("(c p t) n -> p c t n", c=PASSES, t=PACK)
+        for c in range(PASSES):
+            nc.sync.dma_start(out=w2_raw[:, c], in_=w2_v[:, c])
+        nc.sync.dma_start(out=b2b[:], in_=bd2.partition_broadcast(P))
+        load_z(2)
+        load_z(3)
+
+        ident = const.tile([P, P], BF16, name="ident")
+        make_identity(nc, ident[:])
+        ones = const.tile([P, 1], F32, name="ones")
+        nc.vector.memset(ones[:], 1.0)
+        w1g = const.tile([P, PASSES, PACK, P], BF16, name="w1g")
+        nc.vector.tensor_copy(out=w1g[:], in_=w1_raw[:].rearrange("l (c p t) -> l c t p", c=PASSES, t=PACK))
+        b1f = const.tile([P, PLANES], F32, name="b1f")
+        nc.vector.tensor_copy(out=b1f[:], in_=b1_raw[:].rearrange("p c t -> p (c t)"))
+        accx = const.tile([P, TILES], F32, name="accx")
+        accs = const.tile([P, TILES], F32, name="accs")
+        junkv = const.tile([P, D], F32, name="junkv")
+        junks = const.tile([P, D], F32, name="junks")
+        w2g = const.tile([P, PASSES, D, PACK], BF16, name="w2g", align_bytes=64)
+        w2c = const.tile([P, PASSES, D], U32, name="w2c", align_bytes=64)
+        w2s = const.tile([P, PASSES, D], U8, name="w2s", align_bytes=64)
+
+        def regroup(dst, src):
+            nc.vector.tensor_copy(
+                out=dst.rearrange("p (c i) t -> p c t i", i=4),
+                in_=src.rearrange("p t (c i) -> p c t i", i=4),
+            )
+
+        def prep_w2_regroup(c):
+            regroup(w2g[:, c], w2_raw[:, c])
+
+        def prep_w2_quant(c):
+            nc.vector.quantize_mx(
+                out=w2c[:, c, :].bitcast(FP8X4), scales=w2s[:, c, :],
+                in_=w2g[:, c].rearrange("p n t -> p (n t)"),
+            )
+
+        st = {}
+
+        def z_tile(i):
+            m = i // Q
+            for m0, n, zt in zch:
+                if m0 <= m < m0 + n:
+                    return zt[:, i - m0 * Q, :]
+            return None
+
+        def stage_t(m):
+            zt_ps = psumt.tile([P, W], BF16, name="zt_ps")
+            for q in range(Q):
+                nc.tensor.transpose(zt_ps[:, q * P:(q + 1) * P], z_tile(m * Q + q), ident[:])
+            zT = work.tile([P, W], BF16, name="zT")
+            nc.scalar.copy(out=zT[:], in_=zt_ps[:])
+            st[("zT", m)] = zT
+
+        def stage_a(m):
+            zT = st[("zT", m)]
+            hd = [work.tile([P, PACK, W], BF16, name="hd%d" % c) for c in range(PASSES)]
+            late = []
+            for j in range(PLANES):
+                c, t = j // PACK, j % PACK
+                ps = psum1.tile([P, W], F32, name="ps1")
+                nc.tensor.matmul(out=ps[:], lhsT=w1g[:, c, t, :], rhs=zT[:], start=True, stop=True)
+                if j >= PLANES - KV[m]:
+                    late.append((hd[c][:, t, :], ps, j))
+                else:
+                    nc.scalar.activation(out=hd[c][:, t, :], in_=ps[:], func=ACT.Relu, bias=b1f[:, j:j + 1], scale=1.0)
+            st[("hd", m)] = hd
+            st[("late", m)] = late
+
+        def stage_av(m):
+            for dst, ps, j in st[("late", m)]:
+                nc.vector.tensor_scalar(out=dst, in0=ps[:], scalar1=b1f[:, j:j + 1], scalar2=0.0,
+                                        op0=ALU.add, op1=ALU.max)
+
+        def stage_r(m):
+            hd = st[("hd", m)]
+            g = [work.tile([P, W, PACK], BF16, name="g%d" % c, align_bytes=64) for c in range(PASSES)]
+            for c in range(PASSES):
+                regroup(g[c][:], hd[c][:])
+            st[("g", m)] = g
+
+        def stage_q(m):
+            g = st[("g", m)]
+            cs = []
+            for c in range(PASSES):
+                codes = work.tile([P, W], U32, name="codes%d" % c, align_bytes=64)
+                sc = work.tile([P, W], U8, name="sc%d" % c, align_bytes=64)
+                nc.vector.quantize_mx(out=codes[:].bitcast(FP8X4), scales=sc[:], in_=g[c][:].rearrange("p w t -> p (w t)"))
+                cs.append((codes, sc))
+            st[("cs", m)] = cs
+
+        def stage_m(m):
+            cs = st[("cs", m)]
+            v = work.tile([P, Q, D], F32, name="v", bufs=NV)
+            for q in range(Q):
+                ps = psum2.tile([P, D], F32, name="ps2")
+                for c in range(PASSES):
+                    codes, sc = cs[c]
+                    nc.tensor.matmul_mx(
+                        out=ps[:],
+                        lhsT=codes[:, q * P:(q + 1) * P].bitcast(FP8X4), lhsT_scale=sc[:, q * P:(q + 1) * P],
+                        rhs=w2c[:, c, :].bitcast(FP8X4), rhs_scale=w2s[:, c, :],
+                        start=(c == 0), stop=(c == PASSES - 1),
+                    )
+                nc.vector.tensor_tensor(out=v[:, q, :], in0=ps[:], in1=b2b[:], op=ALU.add)
+            st[("v", m)] = v
+
+        def load_x(m):
+            xt = work.tile([P, Q, D], BF16, name="xt", bufs=NX)
+            nc.sync.dma_start(out=xt[:], in_=x_v[:, m * Q:(m + 1) * Q, :])
+            st[("x", m)] = xt
+
+        def stage_d(m):
+            v = st[("v", m)]
+            xt = st[("x", m)]
+            for q in range(Q):
+                i = m * Q + q
+                nc.vector.scalar_tensor_tensor(out=junkv[:], in0=v[:, q, :], scalar=1.0, in1=xt[:, q, :],
+                                               op0=ALU.mult, op1=ALU.mult, accum_out=accx[:, i:i + 1])
+
+        def stage_x(m):
+            v = st[("v", m)]
+            e = work.tile([P, Q, D], F32, name="e", bufs=NE)
+            nc.scalar.activation(out=e[:].rearrange("p q d -> p (q d)"), in_=v[:].rearrange("p q d -> p (q d)"), func=ACT.Exp)
+            st[("e", m)] = e
+
+        def stage_l(m):
+            e = st[("e", m)]
+            for q in range(Q):
+                i = m * Q + q
+                nc.scalar.activation(out=junks[:], in_=e[:, q, :], func=ACT.Ln, bias=ones[:], scale=1.0,
+                                     accum_out=accs[:, i:i + 1])
+
+        jobs = []
+        m0 = 0
+        for n in GROUPS:
+            jobs.extend([("x", m) for m in range(m0, m0 + n)])
+            jobs.extend([("l", m) for m in range(m0, m0 + n)])
+            m0 += n
+        jp = 0
+
+        def ok(m):
+            return 0 <= m < MACROS
+
+        stage_t(0)
+        it = -4
+        while it < MACROS + DLAG or jp < len(jobs):
+            if ok(it + 2):
+                stage_av(it + 2)
+            if ok(it + 1):
+                stage_q(it + 1)
+            if it == -3:
+                prep_w2_regroup(0)
+                prep_w2_regroup(1)
+            if it == -2:
+                prep_w2_quant(0)
+                prep_w2_quant(1)
+            if ok(it):
+                stage_m(it)
+            cap = JPI[it] if 0 <= it < len(JPI) else (100 if it >= len(JPI) else 0)
+            while cap > 0 and jp < len(jobs):
+                kind, m = jobs[jp]
+                if kind == "x" and m > it - XLAG:
+                    break
+                if kind == "x":
+                    stage_x(m)
+                else:
+                    stage_l(m)
+                jp += 1
+                cap -= 1
+            if ok(it + 4) and it + 4 >= 1:
+                stage_t(it + 4)
+            if ok(it - DLAG + 2):
+                load_x(it - DLAG + 2)
+            if ok(it + 3):
+                stage_a(it + 3)
+            if ok(it + 2):
+                stage_r(it + 2)
+            if ok(it - DLAG):
+                stage_d(it - DLAG)
+            it += 1
+
+        res = const.tile([P, TILES], F32, name="res")
+        nc.vector.tensor_sub(out=res[:], in0=accx[:], in1=accs[:])
+        nc.sync.dma_start(out=out_v, in_=res[:])

@@ -24,13 +24,17 @@ FLOPS = 2 * B * (L * H + H * D)
 
 GROUPS = [6, 6, 4]
 DLAG = 5
-KV = [2] * 16
+KV = [1, 1, 1, 3, 3, 3, 2, 2, 3, 3, 3, 3, 2, 2, 3, 3]
 JPI = [0, 1, 1, 2, 2, 2, 2, 2, 2, 2, 2, 2, 2]
 XLAG = 1
 NV = 7
 NE = 8
 NX = 3
 ZCH = [1, 3, 4, 8]
+GUNIT = True
+GSPLIT = 1
+BETA = []
+PRE = 3
 
 
 def tile_vae_pb_t_kernel(tc, z, x, Wd1, bd1, Wd2, bd2, out):
@@ -52,16 +56,21 @@ def tile_vae_pb_t_kernel(tc, z, x, Wd1, bd1, Wd2, bd2, out):
             zt = const.tile([P, n * Q, L], BF16, name="zc%d" % k)
             zch.append((m0, n, zt))
             m0 += n
+
         def load_z(k):
-            m0, n, zt = zch[k]
-            nc.sync.dma_start(out=zt[:], in_=z_v[:, m0 * Q:(m0 + n) * Q, :])
+            a, n, zt = zch[k]
+            nc.sync.dma_start(out=zt[:], in_=z_v[:, a * Q:(a + n) * Q, :])
+
         w1_raw = const.tile([P, H], BF16, name="w1_raw")
-        b1_raw = const.tile([P, PASSES, PACK], BF16, name="b1_raw")
+        b1_pad = const.tile([P, P], BF16, name="b1_pad")
         w2_raw = const.tile([P, PASSES, PACK, D], BF16, name="w2_raw")
         b2b = const.tile([P, D], BF16, name="b2b")
+        if BETA:
+            nc.vector.memset(b1_pad[:], 0.0)
         load_z(0)
         nc.sync.dma_start(out=w1_raw[:], in_=Wd1)
-        nc.sync.dma_start(out=b1_raw[:], in_=bd1.rearrange("(c p t) -> p c t", c=PASSES, t=PACK))
+        nc.sync.dma_start(out=b1_pad[:, 0:PLANES].rearrange("p (c t) -> p c t", c=PASSES),
+                          in_=bd1.rearrange("(c p t) -> p c t", c=PASSES, t=PACK))
         load_z(1)
         w2_v = Wd2.rearrange("(c p t) n -> p c t n", c=PASSES, t=PACK)
         for c in range(PASSES):
@@ -77,7 +86,7 @@ def tile_vae_pb_t_kernel(tc, z, x, Wd1, bd1, Wd2, bd2, out):
         w1g = const.tile([P, PASSES, PACK, P], BF16, name="w1g")
         nc.vector.tensor_copy(out=w1g[:], in_=w1_raw[:].rearrange("l (c p t) -> l c t p", c=PASSES, t=PACK))
         b1f = const.tile([P, PLANES], F32, name="b1f")
-        nc.vector.tensor_copy(out=b1f[:], in_=b1_raw[:].rearrange("p c t -> p (c t)"))
+        nc.vector.tensor_copy(out=b1f[:], in_=b1_pad[:, 0:PLANES])
         accx = const.tile([P, TILES], F32, name="accx")
         accs = const.tile([P, TILES], F32, name="accs")
         junkv = const.tile([P, D], F32, name="junkv")
@@ -85,6 +94,15 @@ def tile_vae_pb_t_kernel(tc, z, x, Wd1, bd1, Wd2, bd2, out):
         w2g = const.tile([P, PASSES, D, PACK], BF16, name="w2g", align_bytes=64)
         w2c = const.tile([P, PASSES, D], U32, name="w2c", align_bytes=64)
         w2s = const.tile([P, PASSES, D], U8, name="w2s", align_bytes=64)
+        bst = None
+        sel = None
+        if BETA:
+            bst = const.tile([P, P], BF16, name="bst")
+            sel = const.tile([P, PLANES, P], BF16, name="sel")
+            nc.vector.tensor_copy(out=sel[:], in_=ident[:, 0:PLANES].unsqueeze(2).to_broadcast([P, PLANES, P]))
+            bt_ps = psumt.tile([P, P], BF16, name="zt_ps")
+            nc.tensor.transpose(bt_ps[:], b1_pad[:], ident[:])
+            nc.scalar.copy(out=bst[:], in_=bt_ps[:])
 
         def regroup(dst, src):
             nc.vector.tensor_copy(
@@ -105,59 +123,93 @@ def tile_vae_pb_t_kernel(tc, z, x, Wd1, bd1, Wd2, bd2, out):
 
         def z_tile(i):
             m = i // Q
-            for m0, n, zt in zch:
-                if m0 <= m < m0 + n:
-                    return zt[:, i - m0 * Q, :]
+            for a, n, zt in zch:
+                if a <= m < a + n:
+                    return zt[:, i - a * Q, :]
             return None
 
         def stage_t(m):
             zt_ps = psumt.tile([P, W], BF16, name="zt_ps")
             for q in range(Q):
                 nc.tensor.transpose(zt_ps[:, q * P:(q + 1) * P], z_tile(m * Q + q), ident[:])
+            st[("zt_ps", m)] = zt_ps
+
+        def stage_tc(m):
             zT = work.tile([P, W], BF16, name="zT")
-            nc.scalar.copy(out=zT[:], in_=zt_ps[:])
+            nc.scalar.copy(out=zT[:], in_=st[("zt_ps", m)][:])
             st[("zT", m)] = zT
 
-        def stage_a(m):
+        def a_begin(m):
+            st[("hd", m)] = [work.tile([P, PACK, W], BF16, name="hd%d" % c) for c in range(PASSES)]
+            st[("late", m)] = []
+            if m in BETA:
+                st[("g1", m)] = work.tile([P, W, PACK], BF16, name="g1", bufs=3, align_bytes=64)
+
+        def a_bank(m, j):
             zT = st[("zT", m)]
-            hd = [work.tile([P, PACK, W], BF16, name="hd%d" % c) for c in range(PASSES)]
-            late = []
-            for j in range(PLANES):
-                c, t = j // PACK, j % PACK
-                ps = psum1.tile([P, W], F32, name="ps1")
+            hd = st[("hd", m)]
+            c, t = j // PACK, j % PACK
+            ps = psum1.tile([P, W], F32, name="ps1")
+            late = j >= PLANES - KV[m]
+            if c == 1 and m in BETA:
+                psv = ps[:].rearrange("p (t r) -> p t r", t=PACK)
+                for u in range(PACK):
+                    nc.tensor.matmul(out=psv[:, u, :], lhsT=bst[:], rhs=sel[:, c * PACK + u, :], start=True, stop=False)
+                    nc.tensor.matmul(out=psv[:, u, :], lhsT=w1g[:, c, u, :], rhs=zT[:, t * P:(t + 1) * P], start=False, stop=True)
+                dst = st[("g1", m)][:, t * P:(t + 1) * P, :]
+                src = ps[:].rearrange("p (t r) -> p r t", t=PACK)
+                if late:
+                    st[("late", m)].append((dst, src, None))
+                else:
+                    nc.scalar.activation(out=dst, in_=src, func=ACT.Relu)
+            else:
                 nc.tensor.matmul(out=ps[:], lhsT=w1g[:, c, t, :], rhs=zT[:], start=True, stop=True)
-                if j >= PLANES - KV[m]:
-                    late.append((hd[c][:, t, :], ps, j))
+                if late:
+                    st[("late", m)].append((hd[c][:, t, :], ps[:], j))
                 else:
                     nc.scalar.activation(out=hd[c][:, t, :], in_=ps[:], func=ACT.Relu, bias=b1f[:, j:j + 1], scale=1.0)
-            st[("hd", m)] = hd
-            st[("late", m)] = late
 
         def stage_av(m):
-            for dst, ps, j in st[("late", m)]:
-                nc.vector.tensor_scalar(out=dst, in0=ps[:], scalar1=b1f[:, j:j + 1], scalar2=0.0,
-                                        op0=ALU.add, op1=ALU.max)
+            for dst, src, j in st[("late", m)]:
+                if j is None:
+                    nc.vector.tensor_scalar(out=dst, in0=src, scalar1=0.0, scalar2=None, op0=ALU.max)
+                else:
+                    nc.vector.tensor_scalar(out=dst, in0=src, scalar1=b1f[:, j:j + 1], scalar2=0.0,
+                                            op0=ALU.add, op1=ALU.max)
+
+        def stage_rg(m):
+            hd = st[("hd", m)]
+            g0 = work.tile([P, W, PACK], BF16, name="g0", bufs=(1 if GUNIT else 2), align_bytes=64)
+            st[("g0", m)] = g0
+            if GUNIT:
+                n = W // GSPLIT
+                for s in range(GSPLIT):
+                    nc.gpsimd.tensor_scalar(out=g0[:, s * n:(s + 1) * n, :],
+                                            in0=hd[0][:, :, s * n:(s + 1) * n].rearrange("p t w -> p w t"),
+                                            scalar1=1.0, scalar2=0.0, op0=ALU.mult, op1=ALU.add)
 
         def stage_r(m):
             hd = st[("hd", m)]
-            g = [work.tile([P, W, PACK], BF16, name="g%d" % c, align_bytes=64) for c in range(PASSES)]
-            for c in range(PASSES):
-                regroup(g[c][:], hd[c][:])
-            st[("g", m)] = g
+            if not GUNIT:
+                regroup(st[("g0", m)][:], hd[0][:])
+            if m not in BETA:
+                g1 = work.tile([P, W, PACK], BF16, name="g1", bufs=3, align_bytes=64)
+                st[("g1", m)] = g1
+                regroup(g1[:], hd[1][:])
 
         def stage_q(m):
-            g = st[("g", m)]
             cs = []
             for c in range(PASSES):
+                g = st[("g%d" % c, m)]
                 codes = work.tile([P, W], U32, name="codes%d" % c, align_bytes=64)
                 sc = work.tile([P, W], U8, name="sc%d" % c, align_bytes=64)
-                nc.vector.quantize_mx(out=codes[:].bitcast(FP8X4), scales=sc[:], in_=g[c][:].rearrange("p w t -> p (w t)"))
+                nc.vector.quantize_mx(out=codes[:].bitcast(FP8X4), scales=sc[:], in_=g[:].rearrange("p w t -> p (w t)"))
                 cs.append((codes, sc))
             st[("cs", m)] = cs
 
-        def stage_m(m):
+        def stage_mx(m):
             cs = st[("cs", m)]
-            v = work.tile([P, Q, D], F32, name="v", bufs=NV)
+            pss = []
             for q in range(Q):
                 ps = psum2.tile([P, D], F32, name="ps2")
                 for c in range(PASSES):
@@ -168,7 +220,13 @@ def tile_vae_pb_t_kernel(tc, z, x, Wd1, bd1, Wd2, bd2, out):
                         rhs=w2c[:, c, :].bitcast(FP8X4), rhs_scale=w2s[:, c, :],
                         start=(c == 0), stop=(c == PASSES - 1),
                     )
-                nc.vector.tensor_tensor(out=v[:, q, :], in0=ps[:], in1=b2b[:], op=ALU.add)
+                pss.append(ps)
+            st[("ps2", m)] = pss
+
+        def stage_va(m):
+            v = work.tile([P, Q, D], F32, name="v", bufs=NV)
+            for q in range(Q):
+                nc.vector.tensor_tensor(out=v[:, q, :], in0=st[("ps2", m)][q][:], in1=b2b[:], op=ALU.add)
             st[("v", m)] = v
 
         def load_x(m):
@@ -209,20 +267,16 @@ def tile_vae_pb_t_kernel(tc, z, x, Wd1, bd1, Wd2, bd2, out):
             return 0 <= m < MACROS
 
         stage_t(0)
+        stage_tc(0)
         it = -4
         while it < MACROS + DLAG or jp < len(jobs):
             if ok(it + 2):
+                stage_rg(it + 2)
                 stage_av(it + 2)
-            if ok(it + 1):
-                stage_q(it + 1)
-            if it == -3:
-                prep_w2_regroup(0)
-                prep_w2_regroup(1)
-            if it == -2:
-                prep_w2_quant(0)
-                prep_w2_quant(1)
             if ok(it):
-                stage_m(it)
+                stage_va(it)
+            if ok(it + 4) and it + 4 >= 1:
+                stage_t(it + 4)
             cap = JPI[it] if 0 <= it < len(JPI) else (100 if it >= len(JPI) else 0)
             while cap > 0 and jp < len(jobs):
                 kind, m = jobs[jp]
@@ -235,15 +289,30 @@ def tile_vae_pb_t_kernel(tc, z, x, Wd1, bd1, Wd2, bd2, out):
                 jp += 1
                 cap -= 1
             if ok(it + 4) and it + 4 >= 1:
-                stage_t(it + 4)
+                stage_tc(it + 4)
             if ok(it - DLAG + 2):
                 load_x(it - DLAG + 2)
             if ok(it + 3):
-                stage_a(it + 3)
+                a_begin(it + 3)
+                for j in range(PRE):
+                    a_bank(it + 3, j)
+            if ok(it + 1):
+                stage_mx(it + 1)
+            if ok(it + 3):
+                for j in range(PRE, PLANES):
+                    a_bank(it + 3, j)
+            if it == -3:
+                prep_w2_regroup(0)
+                prep_w2_regroup(1)
             if ok(it + 2):
                 stage_r(it + 2)
+            if it == -2:
+                prep_w2_quant(0)
+                prep_w2_quant(1)
             if ok(it - DLAG):
                 stage_d(it - DLAG)
+            if ok(it + 2):
+                stage_q(it + 2)
             it += 1
 
         res = const.tile([P, TILES], F32, name="res")

@@ -89,8 +89,6 @@ def tile_vae_pb_t_kernel(tc, z, x, Wd1, bd1, Wd2, bd2, out):
         nc.vector.tensor_copy(out=b1f[:], in_=b1_pad[:, 0:PLANES])
         accx = const.tile([P, TILES], F32, name="accx")
         accs = const.tile([P, TILES], F32, name="accs")
-        junkv = const.tile([P, D], F32, name="junkv")
-        junks = const.tile([P, D], F32, name="junks")
         w2g = const.tile([P, PASSES, D, PACK], BF16, name="w2g", align_bytes=64)
         w2c = const.tile([P, PASSES, D], U32, name="w2c", align_bytes=64)
         w2s = const.tile([P, PASSES, D], U8, name="w2s", align_bytes=64)
@@ -239,6 +237,7 @@ def tile_vae_pb_t_kernel(tc, z, x, Wd1, bd1, Wd2, bd2, out):
             xt = st[("x", m)]
             for q in range(Q):
                 i = m * Q + q
+                junkv = work.tile([P, D], BF16, name="junkv", bufs=4)
                 nc.vector.scalar_tensor_tensor(out=junkv[:], in0=v[:, q, :], scalar=1.0, in1=xt[:, q, :],
                                                op0=ALU.mult, op1=ALU.mult, accum_out=accx[:, i:i + 1])
 
@@ -252,7 +251,7 @@ def tile_vae_pb_t_kernel(tc, z, x, Wd1, bd1, Wd2, bd2, out):
             e = st[("e", m)]
             for q in range(Q):
                 i = m * Q + q
-                nc.scalar.activation(out=junks[:], in_=e[:, q, :], func=ACT.Ln, bias=ones[:], scale=1.0,
+                nc.scalar.activation(out=e[:, q, :], in_=e[:, q, :], func=ACT.Ln, bias=ones[:], scale=1.0,
                                      accum_out=accs[:, i:i + 1])
 
         jobs = []

@@ -23,18 +23,17 @@ PLANES = PASSES * PACK
 FLOPS = 2 * B * (L * H + H * D)
 
 GROUPS = [6, 6, 4]
-DLAG = 5
-KV = [1, 1, 1, 3, 3, 3, 2, 2, 3, 3, 3, 3, 2, 2, 3, 3]
-JPI = [0, 1, 1, 2, 2, 2, 2, 2, 2, 2, 2, 2, 2]
+DLAG = 6
+JPI = [2] * 13
 XLAG = 1
-NV = 7
+NV = 8
 NE = 8
 NX = 3
 ZCH = [1, 3, 4, 8]
-GUNIT = True
-GSPLIT = 1
-BETA = []
-PRE = 3
+NVBS = [2, 2] + [3] * 12 + [4, 4]
+GFROM = 1
+SF = -9
+ZV = [0] * 4 + [1] * 12
 
 
 def tile_vae_pb_t_kernel(tc, z, x, Wd1, bd1, Wd2, bd2, out):
@@ -45,9 +44,8 @@ def tile_vae_pb_t_kernel(tc, z, x, Wd1, bd1, Wd2, bd2, out):
     with ExitStack() as ctx:
         const = ctx.enter_context(tc.tile_pool(name="const", bufs=1))
         work = ctx.enter_context(tc.tile_pool(name="work", bufs=2))
-        psum1 = ctx.enter_context(tc.psum_pool(name="psum1", bufs=3))
-        psum2 = ctx.enter_context(tc.psum_pool(name="psum2", bufs=4))
-        psumt = ctx.enter_context(tc.psum_pool(name="psumt", bufs=1))
+        psum_s = ctx.enter_context(tc.psum_pool(name="psum_s", bufs=3))
+        psum_v = ctx.enter_context(tc.psum_pool(name="psum_v", bufs=5))
         ctx.enter_context(tc.manual_schedule())
 
         zch = []
@@ -65,12 +63,11 @@ def tile_vae_pb_t_kernel(tc, z, x, Wd1, bd1, Wd2, bd2, out):
         b1_pad = const.tile([P, P], BF16, name="b1_pad")
         w2_raw = const.tile([P, PASSES, PACK, D], BF16, name="w2_raw")
         b2b = const.tile([P, D], BF16, name="b2b")
-        if BETA:
-            nc.vector.memset(b1_pad[:], 0.0)
+        nc.vector.memset(b1_pad[:], 0.0)
         load_z(0)
-        nc.sync.dma_start(out=w1_raw[:], in_=Wd1)
         nc.sync.dma_start(out=b1_pad[:, 0:PLANES].rearrange("p (c t) -> p c t", c=PASSES),
                           in_=bd1.rearrange("(c p t) -> p c t", c=PASSES, t=PACK))
+        nc.sync.dma_start(out=w1_raw[:], in_=Wd1)
         load_z(1)
         w2_v = Wd2.rearrange("(c p t) n -> p c t n", c=PASSES, t=PACK)
         for c in range(PASSES):
@@ -83,33 +80,27 @@ def tile_vae_pb_t_kernel(tc, z, x, Wd1, bd1, Wd2, bd2, out):
         make_identity(nc, ident[:])
         ones = const.tile([P, 1], F32, name="ones")
         nc.vector.memset(ones[:], 1.0)
-        w1g = const.tile([P, PASSES, PACK, P], BF16, name="w1g")
-        nc.vector.tensor_copy(out=w1g[:], in_=w1_raw[:].rearrange("l (c p t) -> l c t p", c=PASSES, t=PACK))
+        sel = const.tile([P, PACK, P], BF16, name="sel")
+        nc.vector.tensor_copy(out=sel[:], in_=ident[:, PACK:PLANES].unsqueeze(2).to_broadcast([P, PACK, P]))
         b1f = const.tile([P, PLANES], F32, name="b1f")
         nc.vector.tensor_copy(out=b1f[:], in_=b1_pad[:, 0:PLANES])
+        w1g = const.tile([P, PASSES, PACK, P], BF16, name="w1g")
+        nc.vector.tensor_copy(out=w1g[:], in_=w1_raw[:].rearrange("l (c p t) -> l c t p", c=PASSES, t=PACK))
+        bst = const.tile([P, P], BF16, name="bst")
+        bt_ps = psum_s.tile([P, P], BF16, name="ps1")
+        nc.tensor.transpose(bt_ps[:], b1_pad[:], ident[:])
+        nc.scalar.copy(out=bst[:], in_=bt_ps[:])
         accx = const.tile([P, TILES], F32, name="accx")
         accs = const.tile([P, TILES], F32, name="accs")
         w2g = const.tile([P, PASSES, D, PACK], BF16, name="w2g", align_bytes=64)
         w2c = const.tile([P, PASSES, D], U32, name="w2c", align_bytes=64)
         w2s = const.tile([P, PASSES, D], U8, name="w2s", align_bytes=64)
-        bst = None
-        sel = None
-        if BETA:
-            bst = const.tile([P, P], BF16, name="bst")
-            sel = const.tile([P, PLANES, P], BF16, name="sel")
-            nc.vector.tensor_copy(out=sel[:], in_=ident[:, 0:PLANES].unsqueeze(2).to_broadcast([P, PLANES, P]))
-            bt_ps = psumt.tile([P, P], BF16, name="zt_ps")
-            nc.tensor.transpose(bt_ps[:], b1_pad[:], ident[:])
-            nc.scalar.copy(out=bst[:], in_=bt_ps[:])
-
-        def regroup(dst, src):
-            nc.vector.tensor_copy(
-                out=dst.rearrange("p (c i) t -> p c t i", i=4),
-                in_=src.rearrange("p t (c i) -> p c t i", i=4),
-            )
 
         def prep_w2_regroup(c):
-            regroup(w2g[:, c], w2_raw[:, c])
+            nc.vector.tensor_copy(
+                out=w2g[:, c].rearrange("p (c i) t -> p c t i", i=4),
+                in_=w2_raw[:, c].rearrange("p t (c i) -> p c t i", i=4),
+            )
 
         def prep_w2_quant(c):
             nc.vector.quantize_mx(
@@ -119,6 +110,9 @@ def tile_vae_pb_t_kernel(tc, z, x, Wd1, bd1, Wd2, bd2, out):
 
         st = {}
 
+        def ok(m):
+            return 0 <= m < MACROS
+
         def z_tile(i):
             m = i // Q
             for a, n, zt in zch:
@@ -126,76 +120,143 @@ def tile_vae_pb_t_kernel(tc, z, x, Wd1, bd1, Wd2, bd2, out):
                     return zt[:, i - a * Q, :]
             return None
 
-        def stage_t(m):
-            zt_ps = psumt.tile([P, W], BF16, name="zt_ps")
+        def pe_t(m):
+            if not ok(m):
+                return
+            zt_ps = psum_s.tile([P, W], BF16, name="ps1")
             for q in range(Q):
                 nc.tensor.transpose(zt_ps[:, q * P:(q + 1) * P], z_tile(m * Q + q), ident[:])
             st[("zt_ps", m)] = zt_ps
 
-        def stage_tc(m):
-            zT = work.tile([P, W], BF16, name="zT")
-            nc.scalar.copy(out=zT[:], in_=st[("zt_ps", m)][:])
+        def pe_plane(m, t):
+            if not ok(m):
+                return
+            ps = psum_s.tile([P, W], F32, name="ps1")
+            nc.tensor.matmul(out=ps[:], lhsT=w1g[:, 0, t, :], rhs=st[("zT", m)][:], start=True, stop=True)
+            st[("pl", m, t)] = ps
+
+        def pe_block(m, rb):
+            if not ok(m):
+                return
+            biased = rb >= NVBS[m]
+            pool = psum_s if biased else psum_v
+            ps = pool.tile([P, PACK, P], F32, name=("ps1" if biased else "psv"))
+            zT = st[("zT", m)]
+            for t in range(PACK):
+                if biased:
+                    nc.tensor.matmul(out=ps[:, t, :], lhsT=bst[:], rhs=sel[:, t, :], start=True, stop=False)
+                nc.tensor.matmul(out=ps[:, t, :], lhsT=w1g[:, 1, t, :], rhs=zT[:, rb * P:(rb + 1) * P],
+                                 start=(not biased), stop=True)
+            st[("bl", m, rb)] = ps
+
+        def pe_mx(m, q):
+            cs = st[("cs", m)]
+            ps = psum_v.tile([P, D], F32, name="psv")
+            for c in range(PASSES):
+                codes, sc = cs[c]
+                nc.tensor.matmul_mx(
+                    out=ps[:],
+                    lhsT=codes[:, q * P:(q + 1) * P].bitcast(FP8X4), lhsT_scale=sc[:, q * P:(q + 1) * P],
+                    rhs=w2c[:, c, :].bitcast(FP8X4), rhs_scale=w2s[:, c, :],
+                    start=(c == 0), stop=(c == PASSES - 1),
+                )
+            st[("ps2", m, q)] = ps
+
+        def s_zcopy(m):
+            if not ok(m):
+                return
+            zT = work.tile([P, W], BF16, name="zT", bufs=4)
+            if ZV[m]:
+                nc.vector.tensor_copy(out=zT[:], in_=st[("zt_ps", m)][:])
+            else:
+                nc.scalar.copy(out=zT[:], in_=st[("zt_ps", m)][:])
             st[("zT", m)] = zT
 
-        def a_begin(m):
-            st[("hd", m)] = [work.tile([P, PACK, W], BF16, name="hd%d" % c) for c in range(PASSES)]
-            st[("late", m)] = []
-            if m in BETA:
+        def s_plane(m, t):
+            if not ok(m):
+                return
+            if t == 0:
+                st[("hd0", m)] = work.tile([P, PACK, W], BF16, name="hd0")
+            nc.scalar.activation(out=st[("hd0", m)][:, t, :], in_=st[("pl", m, t)][:], func=ACT.Relu,
+                                 bias=b1f[:, t:t + 1], scale=1.0)
+
+        def g1_of(m):
+            if ("g1", m) not in st:
                 st[("g1", m)] = work.tile([P, W, PACK], BF16, name="g1", bufs=3, align_bytes=64)
+            return st[("g1", m)]
 
-        def a_bank(m, j):
-            zT = st[("zT", m)]
-            hd = st[("hd", m)]
-            c, t = j // PACK, j % PACK
-            ps = psum1.tile([P, W], F32, name="ps1")
-            late = j >= PLANES - KV[m]
-            if c == 1 and m in BETA:
-                psv = ps[:].rearrange("p (t r) -> p t r", t=PACK)
-                for u in range(PACK):
-                    nc.tensor.matmul(out=psv[:, u, :], lhsT=bst[:], rhs=sel[:, c * PACK + u, :], start=True, stop=False)
-                    nc.tensor.matmul(out=psv[:, u, :], lhsT=w1g[:, c, u, :], rhs=zT[:, t * P:(t + 1) * P], start=False, stop=True)
-                dst = st[("g1", m)][:, t * P:(t + 1) * P, :]
-                src = ps[:].rearrange("p (t r) -> p r t", t=PACK)
-                if late:
-                    st[("late", m)].append((dst, src, None))
-                else:
-                    nc.scalar.activation(out=dst, in_=src, func=ACT.Relu)
-            else:
-                nc.tensor.matmul(out=ps[:], lhsT=w1g[:, c, t, :], rhs=zT[:], start=True, stop=True)
-                if late:
-                    st[("late", m)].append((hd[c][:, t, :], ps[:], j))
-                else:
-                    nc.scalar.activation(out=hd[c][:, t, :], in_=ps[:], func=ACT.Relu, bias=b1f[:, j:j + 1], scale=1.0)
+        def s_block(m, rb):
+            if not ok(m):
+                return
+            nc.scalar.activation(out=g1_of(m)[:, rb * P:(rb + 1) * P, :],
+                                 in_=st[("bl", m, rb)][:].rearrange("p t r -> p r t"), func=ACT.Relu)
 
-        def stage_av(m):
-            for dst, src, j in st[("late", m)]:
-                if j is None:
-                    nc.vector.tensor_scalar(out=dst, in0=src, scalar1=0.0, scalar2=None, op0=ALU.max)
-                else:
-                    nc.vector.tensor_scalar(out=dst, in0=src, scalar1=b1f[:, j:j + 1], scalar2=0.0,
-                                            op0=ALU.add, op1=ALU.max)
+        def s_x(m):
+            v = st[("v", m)]
+            e = work.tile([P, Q, D], F32, name="e", bufs=NE)
+            nc.scalar.activation(out=e[:].rearrange("p q d -> p (q d)"), in_=v[:].rearrange("p q d -> p (q d)"), func=ACT.Exp)
+            st[("e", m)] = e
 
-        def stage_rg(m):
-            hd = st[("hd", m)]
-            g0 = work.tile([P, W, PACK], BF16, name="g0", bufs=(1 if GUNIT else 2), align_bytes=64)
+        def s_l(m):
+            e = st[("e", m)]
+            for q in range(Q):
+                i = m * Q + q
+                nc.scalar.activation(out=e[:, q, :], in_=e[:, q, :], func=ACT.Ln, bias=ones[:], scale=1.0,
+                                     accum_out=accs[:, i:i + 1])
+
+        def g_regroup(m):
+            if not ok(m):
+                return
+            g0 = work.tile([P, W, PACK], BF16, name="g0", bufs=1, align_bytes=64)
             st[("g0", m)] = g0
-            if GUNIT:
-                n = W // GSPLIT
-                for s in range(GSPLIT):
-                    nc.gpsimd.tensor_scalar(out=g0[:, s * n:(s + 1) * n, :],
-                                            in0=hd[0][:, :, s * n:(s + 1) * n].rearrange("p t w -> p w t"),
-                                            scalar1=1.0, scalar2=0.0, op0=ALU.mult, op1=ALU.add)
+            if m >= GFROM:
+                nc.gpsimd.tensor_scalar(out=g0[:], in0=st[("hd0", m)][:].rearrange("p t w -> p w t"),
+                                        scalar1=1.0, scalar2=0.0, op0=ALU.mult, op1=ALU.add)
 
-        def stage_r(m):
-            hd = st[("hd", m)]
-            if not GUNIT:
-                regroup(st[("g0", m)][:], hd[0][:])
-            if m not in BETA:
-                g1 = work.tile([P, W, PACK], BF16, name="g1", bufs=3, align_bytes=64)
-                st[("g1", m)] = g1
-                regroup(g1[:], hd[1][:])
+        def v_regroup(m):
+            if not ok(m) or m >= GFROM:
+                return
+            nc.vector.tensor_copy(
+                out=st[("g0", m)][:].rearrange("p (c i) t -> p c t i", i=4),
+                in_=st[("hd0", m)][:].rearrange("p t (c i) -> p c t i", i=4),
+            )
 
-        def stage_q(m):
+        def v_block(m, rb):
+            if not ok(m):
+                return
+            nc.vector.tensor_tensor(out=g1_of(m)[:, rb * P:(rb + 1) * P, :],
+                                    in0=st[("bl", m, rb)][:].rearrange("p t r -> p r t"),
+                                    in1=b1f[:, PACK:PLANES].unsqueeze(1).to_broadcast([P, P, PACK]), op=ALU.add)
+
+        def v_relu(m):
+            if not ok(m):
+                return
+            if NVBS[m] == 0:
+                return
+            part = g1_of(m)[:, 0:NVBS[m] * P, :]
+            nc.vector.tensor_scalar(out=part, in0=part, scalar1=0.0, scalar2=None, op0=ALU.max)
+
+        def v_a(m, q):
+            if not ok(m):
+                return
+            if q == 0:
+                st[("v", m)] = work.tile([P, Q, D], F32, name="v", bufs=NV)
+            nc.vector.tensor_tensor(out=st[("v", m)][:, q, :], in0=st[("ps2", m, q)][:], in1=b2b[:], op=ALU.add)
+
+        def v_d(m):
+            if not ok(m):
+                return
+            v = st[("v", m)]
+            xt = st[("x", m)]
+            for q in range(Q):
+                i = m * Q + q
+                junkv = work.tile([P, D], BF16, name="junkv", bufs=4)
+                nc.vector.scalar_tensor_tensor(out=junkv[:], in0=v[:, q, :], scalar=1.0, in1=xt[:, q, :],
+                                               op0=ALU.mult, op1=ALU.mult, accum_out=accx[:, i:i + 1])
+
+        def v_q(m):
+            if not ok(m):
+                return
             cs = []
             for c in range(PASSES):
                 g = st[("g%d" % c, m)]
@@ -205,54 +266,12 @@ def tile_vae_pb_t_kernel(tc, z, x, Wd1, bd1, Wd2, bd2, out):
                 cs.append((codes, sc))
             st[("cs", m)] = cs
 
-        def stage_mx(m):
-            cs = st[("cs", m)]
-            pss = []
-            for q in range(Q):
-                ps = psum2.tile([P, D], F32, name="ps2")
-                for c in range(PASSES):
-                    codes, sc = cs[c]
-                    nc.tensor.matmul_mx(
-                        out=ps[:],
-                        lhsT=codes[:, q * P:(q + 1) * P].bitcast(FP8X4), lhsT_scale=sc[:, q * P:(q + 1) * P],
-                        rhs=w2c[:, c, :].bitcast(FP8X4), rhs_scale=w2s[:, c, :],
-                        start=(c == 0), stop=(c == PASSES - 1),
-                    )
-                pss.append(ps)
-            st[("ps2", m)] = pss
-
-        def stage_va(m):
-            v = work.tile([P, Q, D], F32, name="v", bufs=NV)
-            for q in range(Q):
-                nc.vector.tensor_tensor(out=v[:, q, :], in0=st[("ps2", m)][q][:], in1=b2b[:], op=ALU.add)
-            st[("v", m)] = v
-
         def load_x(m):
+            if not ok(m):
+                return
             xt = work.tile([P, Q, D], BF16, name="xt", bufs=NX)
             nc.sync.dma_start(out=xt[:], in_=x_v[:, m * Q:(m + 1) * Q, :])
             st[("x", m)] = xt
-
-        def stage_d(m):
-            v = st[("v", m)]
-            xt = st[("x", m)]
-            for q in range(Q):
-                i = m * Q + q
-                junkv = work.tile([P, D], BF16, name="junkv", bufs=4)
-                nc.vector.scalar_tensor_tensor(out=junkv[:], in0=v[:, q, :], scalar=1.0, in1=xt[:, q, :],
-                                               op0=ALU.mult, op1=ALU.mult, accum_out=accx[:, i:i + 1])
-
-        def stage_x(m):
-            v = st[("v", m)]
-            e = work.tile([P, Q, D], F32, name="e", bufs=NE)
-            nc.scalar.activation(out=e[:].rearrange("p q d -> p (q d)"), in_=v[:].rearrange("p q d -> p (q d)"), func=ACT.Exp)
-            st[("e", m)] = e
-
-        def stage_l(m):
-            e = st[("e", m)]
-            for q in range(Q):
-                i = m * Q + q
-                nc.scalar.activation(out=e[:, q, :], in_=e[:, q, :], func=ACT.Ln, bias=ones[:], scale=1.0,
-                                     accum_out=accs[:, i:i + 1])
 
         jobs = []
         m0 = 0
@@ -262,56 +281,113 @@ def tile_vae_pb_t_kernel(tc, z, x, Wd1, bd1, Wd2, bd2, out):
             m0 += n
         jp = 0
 
-        def ok(m):
-            return 0 <= m < MACROS
+        sitems = []
+        for r in range(-4, MACROS):
+            if ok(r + 4):
+                sitems.append(("z", r + 4, 0, r))
+            if ok(r + 3):
+                for t in range(PACK):
+                    sitems.append(("p", r + 3, t, r))
+                for rb in range(NVBS[r + 3], Q):
+                    sitems.append(("b", r + 3, rb, r))
+        vitems = []
+        for r in range(-2, MACROS):
+            if ok(r):
+                for q in range(Q):
+                    vitems.append(("a", r, q, r))
+            if ok(r + 2):
+                for rb in range(NVBS[r + 2]):
+                    vitems.append(("b", r + 2, rb, r))
 
-        stage_t(0)
-        stage_tc(0)
+        ptr = {"sp": 0, "sf": 0, "vp": 0, "vf": 0}
+
+        def fill_s():
+            while ptr["sf"] < len(sitems) and ptr["sf"] < ptr["sp"] + 3:
+                kind, m, k, r = sitems[ptr["sf"]]
+                if kind != "z" and ("zT", m) not in st:
+                    break
+                if kind == "z":
+                    pe_t(m)
+                elif kind == "p":
+                    pe_plane(m, k)
+                else:
+                    pe_block(m, k)
+                ptr["sf"] += 1
+
+        def fill_v():
+            while ptr["vf"] < len(vitems) and ptr["vf"] < ptr["vp"] + 5:
+                kind, m, k, r = vitems[ptr["vf"]]
+                if kind == "a":
+                    if ("cs", m) not in st:
+                        break
+                    pe_mx(m, k)
+                else:
+                    if ("zT", m) not in st:
+                        break
+                    pe_block(m, k)
+                ptr["vf"] += 1
+
+        fill_s()
         it = -4
         while it < MACROS + DLAG or jp < len(jobs):
-            if ok(it + 2):
-                stage_rg(it + 2)
-                stage_av(it + 2)
-            if ok(it):
-                stage_va(it)
-            if ok(it + 4) and it + 4 >= 1:
-                stage_t(it + 4)
+            if it < SF:
+                while ptr["sp"] < len(sitems) and sitems[ptr["sp"]][3] == it:
+                    kind, m, k, r = sitems[ptr["sp"]]
+                    if kind == "z":
+                        s_zcopy(m)
+                    elif kind == "p":
+                        s_plane(m, k)
+                    else:
+                        s_block(m, k)
+                    ptr["sp"] += 1
+                    fill_s()
+            g_regroup(it + 2)
+            fill_v()
+            while ptr["vp"] < len(vitems) and vitems[ptr["vp"]][3] == it:
+                kind, m, k, r = vitems[ptr["vp"]]
+                if kind == "a":
+                    v_a(m, k)
+                else:
+                    v_block(m, k)
+                ptr["vp"] += 1
+                fill_v()
+            if ptr["sp"] < len(sitems) and sitems[ptr["sp"]][3] == it and sitems[ptr["sp"]][0] == "z" and ZV[sitems[ptr["sp"]][1]]:
+                s_zcopy(sitems[ptr["sp"]][1])
+                ptr["sp"] += 1
+                fill_s()
             cap = JPI[it] if 0 <= it < len(JPI) else (100 if it >= len(JPI) else 0)
             while cap > 0 and jp < len(jobs):
                 kind, m = jobs[jp]
                 if kind == "x" and m > it - XLAG:
                     break
                 if kind == "x":
-                    stage_x(m)
+                    s_x(m)
                 else:
-                    stage_l(m)
+                    s_l(m)
                 jp += 1
                 cap -= 1
-            if ok(it + 4) and it + 4 >= 1:
-                stage_tc(it + 4)
-            if ok(it - DLAG + 2):
-                load_x(it - DLAG + 2)
-            if ok(it + 3):
-                a_begin(it + 3)
-                for j in range(PRE):
-                    a_bank(it + 3, j)
-            if ok(it + 1):
-                stage_mx(it + 1)
-            if ok(it + 3):
-                for j in range(PRE, PLANES):
-                    a_bank(it + 3, j)
-            if it == -3:
+            load_x(it - DLAG + 2)
+            while ptr["sp"] < len(sitems) and sitems[ptr["sp"]][3] == it:
+                kind, m, k, r = sitems[ptr["sp"]]
+                if kind == "z":
+                    s_zcopy(m)
+                elif kind == "p":
+                    s_plane(m, k)
+                else:
+                    s_block(m, k)
+                ptr["sp"] += 1
+                fill_s()
+            if it == -4:
                 prep_w2_regroup(0)
                 prep_w2_regroup(1)
-            if ok(it + 2):
-                stage_r(it + 2)
-            if it == -2:
+            v_regroup(it + 2)
+            v_relu(it + 2)
+            if it == -3:
                 prep_w2_quant(0)
                 prep_w2_quant(1)
-            if ok(it - DLAG):
-                stage_d(it - DLAG)
-            if ok(it + 2):
-                stage_q(it + 2)
+            v_d(it - DLAG)
+            v_q(it + 2)
+            fill_v()
             it += 1
 
         res = const.tile([P, TILES], F32, name="res")

@@ -44,8 +44,8 @@ def tile_vae_pb_t_kernel(tc, z, x, Wd1, bd1, Wd2, bd2, out):
     with ExitStack() as ctx:
         const = ctx.enter_context(tc.tile_pool(name="const", bufs=1))
         work = ctx.enter_context(tc.tile_pool(name="work", bufs=2))
-        psum_s = ctx.enter_context(tc.psum_pool(name="psum_s", bufs=3))
-        psum_v = ctx.enter_context(tc.psum_pool(name="psum_v", bufs=5))
+        psum_s = ctx.enter_context(tc.psum_pool(name="psum_s", bufs=4))
+        psum_v = ctx.enter_context(tc.psum_pool(name="psum_v", bufs=4))
         ctx.enter_context(tc.manual_schedule())
 
         zch = []
@@ -302,7 +302,7 @@ def tile_vae_pb_t_kernel(tc, z, x, Wd1, bd1, Wd2, bd2, out):
         ptr = {"sp": 0, "sf": 0, "vp": 0, "vf": 0}
 
         def fill_s():
-            while ptr["sf"] < len(sitems) and ptr["sf"] < ptr["sp"] + 3:
+            while ptr["sf"] < len(sitems) and ptr["sf"] < ptr["sp"] + 4:
                 kind, m, k, r = sitems[ptr["sf"]]
                 if kind != "z" and ("zT", m) not in st:
                     break
@@ -315,7 +315,7 @@ def tile_vae_pb_t_kernel(tc, z, x, Wd1, bd1, Wd2, bd2, out):
                 ptr["sf"] += 1
 
         def fill_v():
-            while ptr["vf"] < len(vitems) and ptr["vf"] < ptr["vp"] + 5:
+            while ptr["vf"] < len(vitems) and ptr["vf"] < ptr["vp"] + 4:
                 kind, m, k, r = vitems[ptr["vf"]]
                 if kind == "a":
                     if ("cs", m) not in st:

@@ -30,7 +30,7 @@ NV = 8
 NE = 8
 NX = 3
 ZCH = [1, 3, 4, 8]
-NVBS = [2, 2] + [3] * 12 + [4, 4]
+NVBS = [2] * 8 + [3] * 6 + [4, 4]
 GFROM = 1
 SF = -9
 ZV = [0] * 4 + [1] * 12

@@ -32,6 +32,7 @@ NX = 3
 ZCH = [1, 3, 4, 8]
 NVBS = [2] * 8 + [3] * 6 + [4, 4]
 GFROM = 1
+WARM = 6
 SF = -9
 ZV = [0] * 4 + [1] * 12
 
@@ -64,6 +65,8 @@ def tile_vae_pb_t_kernel(tc, z, x, Wd1, bd1, Wd2, bd2, out):
         w2_raw = const.tile([P, PASSES, PACK, D], BF16, name="w2_raw")
         b2b = const.tile([P, D], BF16, name="b2b")
         nc.vector.memset(b1_pad[:], 0.0)
+        warm = const.tile([P, W], BF16, name="warm")
+        nc.vector.memset(warm[:], 0.0)
         load_z(0)
         nc.sync.dma_start(out=b1_pad[:, 0:PLANES].rearrange("p (c t) -> p c t", c=PASSES),
                           in_=bd1.rearrange("(c p t) -> p c t", c=PASSES, t=PACK))
@@ -76,6 +79,9 @@ def tile_vae_pb_t_kernel(tc, z, x, Wd1, bd1, Wd2, bd2, out):
         load_z(2)
         load_z(3)
 
+        warm_ps = psum_v.tile([P, W], F32, name="psv")
+        for k in range(WARM):
+            nc.tensor.matmul(out=warm_ps[:], lhsT=warm[:, 0:P], rhs=warm[:], start=True, stop=True)
         ident = const.tile([P, P], BF16, name="ident")
         make_identity(nc, ident[:])
         ones = const.tile([P, 1], F32, name="ones")

@@ -22,19 +22,27 @@ W = Q * P
 PLANES = PASSES * PACK
 FLOPS = 2 * B * (L * H + H * D)
 
-GROUPS = [6, 6, 4]
-DLAG = 6
-JPI = [2] * 13
+GROUPS = [5, 6, 5]
+DAT = [m + 5 for m in range(16)]
+JPI = [1] * 2 + [2] * 11
 XLAG = 1
-NV = 8
-NE = 8
+SB = 4
+BFIRST = 1
+VORD = "bhaz"
+SMODE = "jr"
+XP = 1
+NV = 7
+NE = 6
 NX = 3
 ZCH = [1, 3, 4, 8]
-NVBS = [2] * 8 + [3] * 6 + [4, 4]
+NVBS = [3] * 8 + [2] * 8
+VBIAS = [0] * 8 + [1] * 8
+NH = 2
+HALF = [0] * 8 + [1] * 8
+SBK = "M" * 11 + "T" * 5
 GFROM = 1
-WARM = 6
 SF = -9
-ZV = [0] * 4 + [1] * 12
+ZV = [0] * 8 + [1] * 8
 
 
 def tile_vae_pb_t_kernel(tc, z, x, Wd1, bd1, Wd2, bd2, out):
@@ -45,8 +53,8 @@ def tile_vae_pb_t_kernel(tc, z, x, Wd1, bd1, Wd2, bd2, out):
     with ExitStack() as ctx:
         const = ctx.enter_context(tc.tile_pool(name="const", bufs=1))
         work = ctx.enter_context(tc.tile_pool(name="work", bufs=2))
-        psum_s = ctx.enter_context(tc.psum_pool(name="psum_s", bufs=4))
-        psum_v = ctx.enter_context(tc.psum_pool(name="psum_v", bufs=4))
+        psum_s = ctx.enter_context(tc.psum_pool(name="psum_s", bufs=SB))
+        psum_v = ctx.enter_context(tc.psum_pool(name="psum_v", bufs=8 - SB))
         ctx.enter_context(tc.manual_schedule())
 
         zch = []
@@ -65,8 +73,6 @@ def tile_vae_pb_t_kernel(tc, z, x, Wd1, bd1, Wd2, bd2, out):
         w2_raw = const.tile([P, PASSES, PACK, D], BF16, name="w2_raw")
         b2b = const.tile([P, D], BF16, name="b2b")
         nc.vector.memset(b1_pad[:], 0.0)
-        warm = const.tile([P, W], BF16, name="warm")
-        nc.vector.memset(warm[:], 0.0)
         load_z(0)
         nc.sync.dma_start(out=b1_pad[:, 0:PLANES].rearrange("p (c t) -> p c t", c=PASSES),
                           in_=bd1.rearrange("(c p t) -> p c t", c=PASSES, t=PACK))
@@ -79,23 +85,29 @@ def tile_vae_pb_t_kernel(tc, z, x, Wd1, bd1, Wd2, bd2, out):
         load_z(2)
         load_z(3)
 
-        warm_ps = psum_v.tile([P, W], F32, name="psv")
-        for k in range(WARM):
-            nc.tensor.matmul(out=warm_ps[:], lhsT=warm[:, 0:P], rhs=warm[:], start=True, stop=True)
         ident = const.tile([P, P], BF16, name="ident")
         make_identity(nc, ident[:])
         ones = const.tile([P, 1], F32, name="ones")
         nc.vector.memset(ones[:], 1.0)
+        identf = const.tile([P, P], F32, name="identf")
+        make_identity(nc, identf[:])
+        selh = const.tile([P, NH, W], BF16, name="selh")
         sel = const.tile([P, PACK, P], BF16, name="sel")
-        nc.vector.tensor_copy(out=sel[:], in_=ident[:, PACK:PLANES].unsqueeze(2).to_broadcast([P, PACK, P]))
         b1f = const.tile([P, PLANES], F32, name="b1f")
         nc.vector.tensor_copy(out=b1f[:], in_=b1_pad[:, 0:PLANES])
         w1g = const.tile([P, PASSES, PACK, P], BF16, name="w1g")
         nc.vector.tensor_copy(out=w1g[:], in_=w1_raw[:].rearrange("l (c p t) -> l c t p", c=PASSES, t=PACK))
         bst = const.tile([P, P], BF16, name="bst")
-        bt_ps = psum_s.tile([P, P], BF16, name="ps1")
+        bt_ps = psum_v.tile([P, P], BF16, name="psv")
         nc.tensor.transpose(bt_ps[:], b1_pad[:], ident[:])
         nc.scalar.copy(out=bst[:], in_=bt_ps[:])
+        bb = const.tile([P, PACK, P], F32, name="bb")
+        bb_ps = psum_v.tile([P, PACK, P], F32, name="psv")
+        for t in range(PACK):
+            nc.tensor.transpose(bb_ps[:, t, :], b1f[:, PACK + t:PACK + t + 1].to_broadcast([P, P]), identf[:])
+        nc.vector.tensor_copy(out=bb[:], in_=bb_ps[:])
+        nc.vector.tensor_copy(out=sel[:], in_=ident[:, PACK:PLANES].unsqueeze(2).to_broadcast([P, PACK, P]))
+        nc.vector.tensor_copy(out=selh[:], in_=ident[:, PACK - NH:PACK].unsqueeze(2).to_broadcast([P, NH, W]))
         accx = const.tile([P, TILES], F32, name="accx")
         accs = const.tile([P, TILES], F32, name="accs")
         w2g = const.tile([P, PASSES, D, PACK], BF16, name="w2g", align_bytes=64)
@@ -126,10 +138,10 @@ def tile_vae_pb_t_kernel(tc, z, x, Wd1, bd1, Wd2, bd2, out):
                     return zt[:, i - a * Q, :]
             return None
 
-        def pe_t(m):
+        def pe_t(m, on_v):
             if not ok(m):
                 return
-            zt_ps = psum_s.tile([P, W], BF16, name="ps1")
+            zt_ps = (psum_v if on_v else psum_s).tile([P, W], BF16, name=("psv" if on_v else "ps1"))
             for q in range(Q):
                 nc.tensor.transpose(zt_ps[:, q * P:(q + 1) * P], z_tile(m * Q + q), ident[:])
             st[("zt_ps", m)] = zt_ps
@@ -144,16 +156,28 @@ def tile_vae_pb_t_kernel(tc, z, x, Wd1, bd1, Wd2, bd2, out):
         def pe_block(m, rb):
             if not ok(m):
                 return
-            biased = rb >= NVBS[m]
-            pool = psum_s if biased else psum_v
-            ps = pool.tile([P, PACK, P], F32, name=("ps1" if biased else "psv"))
+            on_s = rb >= NVBS[m]
+            pool = psum_s if on_s else psum_v
+            ps = pool.tile([P, PACK, P], F32, name=("ps1" if on_s else "psv"))
             zT = st[("zT", m)]
+            biased = on_s or VBIAS[m]
+            if on_s and SBK[m] == "M":
+                nc.tensor.matmul(out=ps[:].rearrange("p t r -> p (t r)"), lhsT=bst[:], rhs=sel[:].rearrange("p t r -> p (t r)"), start=True, stop=False)
+            elif biased:
+                for t in range(PACK):
+                    nc.tensor.matmul(out=ps[:, t, :], lhsT=bb[:, t, :], rhs=identf[:], is_transpose=True,
+                                     start=(t == 0), stop=False)
             for t in range(PACK):
-                if biased:
-                    nc.tensor.matmul(out=ps[:, t, :], lhsT=bst[:], rhs=sel[:, t, :], start=True, stop=False)
                 nc.tensor.matmul(out=ps[:, t, :], lhsT=w1g[:, 1, t, :], rhs=zT[:, rb * P:(rb + 1) * P],
-                                 start=(not biased), stop=True)
+                                 start=(not biased), stop=(not biased or t == PACK - 1))
             st[("bl", m, rb)] = ps
+
+        def pe_half(m):
+            ps = psum_v.tile([P, NH, W], BF16, name="psv")
+            for j in range(NH):
+                nc.tensor.matmul(out=ps[:, j, :], lhsT=bst[:], rhs=selh[:, j, :], start=True, stop=False)
+                nc.tensor.matmul(out=ps[:, j, :], lhsT=w1g[:, 0, PACK - NH + j, :], rhs=st[("zT", m)][:], start=False, stop=True)
+            st[("hf", m)] = ps
 
         def pe_mx(m, q):
             cs = st[("cs", m)]
@@ -178,12 +202,15 @@ def tile_vae_pb_t_kernel(tc, z, x, Wd1, bd1, Wd2, bd2, out):
                 nc.scalar.copy(out=zT[:], in_=st[("zt_ps", m)][:])
             st[("zT", m)] = zT
 
+        def hd0_of(m):
+            if ("hd0", m) not in st:
+                st[("hd0", m)] = work.tile([P, PACK, W], BF16, name="hd0")
+            return st[("hd0", m)]
+
         def s_plane(m, t):
             if not ok(m):
                 return
-            if t == 0:
-                st[("hd0", m)] = work.tile([P, PACK, W], BF16, name="hd0")
-            nc.scalar.activation(out=st[("hd0", m)][:, t, :], in_=st[("pl", m, t)][:], func=ACT.Relu,
+            nc.scalar.activation(out=hd0_of(m)[:, t, :], in_=st[("pl", m, t)][:], func=ACT.Relu,
                                  bias=b1f[:, t:t + 1], scale=1.0)
 
         def g1_of(m):
@@ -197,18 +224,36 @@ def tile_vae_pb_t_kernel(tc, z, x, Wd1, bd1, Wd2, bd2, out):
             nc.scalar.activation(out=g1_of(m)[:, rb * P:(rb + 1) * P, :],
                                  in_=st[("bl", m, rb)][:].rearrange("p t r -> p r t"), func=ACT.Relu)
 
-        def s_x(m):
+        def s_x(m, q):
             v = st[("v", m)]
-            e = work.tile([P, Q, D], F32, name="e", bufs=NE)
-            nc.scalar.activation(out=e[:].rearrange("p q d -> p (q d)"), in_=v[:].rearrange("p q d -> p (q d)"), func=ACT.Exp)
-            st[("e", m)] = e
-
-        def s_l(m):
+            if q <= 0:
+                st[("e", m)] = work.tile([P, Q, D], F32, name="e", bufs=NE)
             e = st[("e", m)]
-            for q in range(Q):
-                i = m * Q + q
-                nc.scalar.activation(out=e[:, q, :], in_=e[:, q, :], func=ACT.Ln, bias=ones[:], scale=1.0,
-                                     accum_out=accs[:, i:i + 1])
+            if q < 0:
+                nc.scalar.activation(out=e[:].rearrange("p q d -> p (q d)"), in_=v[:].rearrange("p q d -> p (q d)"), func=ACT.Exp)
+            else:
+                nc.scalar.activation(out=e[:, q, :], in_=v[:, q, :], func=ACT.Exp)
+
+        def s_l(m, q):
+            e = st[("e", m)]
+            i = m * Q + q
+            nc.scalar.activation(out=e[:, q, :], in_=e[:, q, :], func=ACT.Ln, bias=ones[:], scale=1.0,
+                                 accum_out=accs[:, i:i + 1])
+
+        def order_s(rd, jb):
+            if SMODE == "jr":
+                return jb + rd
+            if SMODE == "rj":
+                return rd + jb
+            seq = []
+            n = len(rd)
+            k = 0
+            for i in range(n):
+                seq.append(rd[i])
+                k2 = (i + 1) * len(jb) // n
+                seq.extend(jb[k:k2])
+                k = k2
+            return seq + jb[k:]
 
         def g_regroup(m):
             if not ok(m):
@@ -230,17 +275,24 @@ def tile_vae_pb_t_kernel(tc, z, x, Wd1, bd1, Wd2, bd2, out):
         def v_block(m, rb):
             if not ok(m):
                 return
-            nc.vector.tensor_tensor(out=g1_of(m)[:, rb * P:(rb + 1) * P, :],
-                                    in0=st[("bl", m, rb)][:].rearrange("p t r -> p r t"),
-                                    in1=b1f[:, PACK:PLANES].unsqueeze(1).to_broadcast([P, P, PACK]), op=ALU.add)
+            if VBIAS[m]:
+                nc.vector.tensor_scalar(out=g1_of(m)[:, rb * P:(rb + 1) * P, :],
+                                        in0=st[("bl", m, rb)][:].rearrange("p t r -> p r t"),
+                                        scalar1=0.0, scalar2=None, op0=ALU.max)
+            else:
+                nc.vector.tensor_tensor(out=g1_of(m)[:, rb * P:(rb + 1) * P, :],
+                                        in0=st[("bl", m, rb)][:].rearrange("p t r -> p r t"),
+                                        in1=b1f[:, PACK:PLANES].unsqueeze(1).to_broadcast([P, P, PACK]), op=ALU.add)
 
         def v_relu(m):
-            if not ok(m):
-                return
-            if NVBS[m] == 0:
+            if not ok(m) or VBIAS[m] or NVBS[m] == 0:
                 return
             part = g1_of(m)[:, 0:NVBS[m] * P, :]
             nc.vector.tensor_scalar(out=part, in0=part, scalar1=0.0, scalar2=None, op0=ALU.max)
+
+        def v_half(m):
+            nc.vector.tensor_scalar(out=hd0_of(m)[:, PACK - NH:PACK, :], in0=st[("hf", m)][:],
+                                    scalar1=0.0, scalar2=None, op0=ALU.max)
 
         def v_a(m, q):
             if not ok(m):
@@ -289,31 +341,31 @@ def tile_vae_pb_t_kernel(tc, z, x, Wd1, bd1, Wd2, bd2, out):
 
         sitems = []
         for r in range(-4, MACROS):
-            if ok(r + 4):
+            if ok(r + 4) and not ZV[r + 4]:
                 sitems.append(("z", r + 4, 0, r))
             if ok(r + 3):
-                for t in range(PACK):
-                    sitems.append(("p", r + 3, t, r))
-                for rb in range(NVBS[r + 3], Q):
-                    sitems.append(("b", r + 3, rb, r))
+                pl = [("p", r + 3, t, r) for t in range(PACK - NH if HALF[r + 3] else PACK)]
+                bl = [("b", r + 3, rb, r) for rb in range(NVBS[r + 3], Q)]
+                sitems.extend(bl + pl if BFIRST and r + 3 > 0 else pl + bl)
         vitems = []
-        for r in range(-2, MACROS):
-            if ok(r):
-                for q in range(Q):
-                    vitems.append(("a", r, q, r))
-            if ok(r + 2):
-                for rb in range(NVBS[r + 2]):
-                    vitems.append(("b", r + 2, rb, r))
+        for r in range(-4, MACROS):
+            h = [("h", r + 3, 0, r)] if ok(r + 3) and HALF[r + 3] else []
+            z = [("z", r + 4, 0, r)] if ok(r + 4) and ZV[r + 4] else []
+            aa = [("a", r, q, r) for q in range(Q)] if ok(r) else []
+            bb_ = [("b", r + 2, rb, r) for rb in range(NVBS[r + 2])] if ok(r + 2) else []
+            d = {"h": h, "z": z, "a": aa, "b": bb_}
+            for k in VORD:
+                vitems.extend(d[k])
 
         ptr = {"sp": 0, "sf": 0, "vp": 0, "vf": 0}
 
         def fill_s():
-            while ptr["sf"] < len(sitems) and ptr["sf"] < ptr["sp"] + 4:
+            while ptr["sf"] < len(sitems) and ptr["sf"] < ptr["sp"] + SB:
                 kind, m, k, r = sitems[ptr["sf"]]
                 if kind != "z" and ("zT", m) not in st:
                     break
                 if kind == "z":
-                    pe_t(m)
+                    pe_t(m, 0)
                 elif kind == "p":
                     pe_plane(m, k)
                 else:
@@ -321,77 +373,98 @@ def tile_vae_pb_t_kernel(tc, z, x, Wd1, bd1, Wd2, bd2, out):
                 ptr["sf"] += 1
 
         def fill_v():
-            while ptr["vf"] < len(vitems) and ptr["vf"] < ptr["vp"] + 4:
+            while ptr["vf"] < len(vitems) and ptr["vf"] < ptr["vp"] + 8 - SB:
                 kind, m, k, r = vitems[ptr["vf"]]
-                if kind == "a":
+                if kind == "z":
+                    pe_t(m, 1)
+                elif kind == "a":
                     if ("cs", m) not in st:
                         break
                     pe_mx(m, k)
                 else:
                     if ("zT", m) not in st:
                         break
-                    pe_block(m, k)
+                    if kind == "h":
+                        pe_half(m)
+                    else:
+                        pe_block(m, k)
                 ptr["vf"] += 1
+
+        def v_one():
+            kind, m, k, r = vitems[ptr["vp"]]
+            if kind == "a":
+                v_a(m, k)
+            elif kind == "h":
+                v_half(m)
+            elif kind == "z":
+                s_zcopy(m)
+            else:
+                v_block(m, k)
+            ptr["vp"] += 1
+            fill_v()
+
+        def s_one():
+            kind, m, k, r = sitems[ptr["sp"]]
+            if kind == "z":
+                s_zcopy(m)
+            elif kind == "p":
+                s_plane(m, k)
+            else:
+                s_block(m, k)
+            ptr["sp"] += 1
+            fill_s()
 
         fill_s()
         it = -4
-        while it < MACROS + DLAG or jp < len(jobs):
-            if it < SF:
-                while ptr["sp"] < len(sitems) and sitems[ptr["sp"]][3] == it:
-                    kind, m, k, r = sitems[ptr["sp"]]
-                    if kind == "z":
-                        s_zcopy(m)
-                    elif kind == "p":
-                        s_plane(m, k)
-                    else:
-                        s_block(m, k)
-                    ptr["sp"] += 1
-                    fill_s()
+        while it <= max(DAT) or jp < len(jobs):
             g_regroup(it + 2)
             fill_v()
-            while ptr["vp"] < len(vitems) and vitems[ptr["vp"]][3] == it:
-                kind, m, k, r = vitems[ptr["vp"]]
-                if kind == "a":
-                    v_a(m, k)
-                else:
-                    v_block(m, k)
-                ptr["vp"] += 1
-                fill_v()
-            if ptr["sp"] < len(sitems) and sitems[ptr["sp"]][3] == it and sitems[ptr["sp"]][0] == "z" and ZV[sitems[ptr["sp"]][1]]:
-                s_zcopy(sitems[ptr["sp"]][1])
-                ptr["sp"] += 1
-                fill_s()
+            fill_s()
+            nv = 0
+            while ptr["vp"] + nv < len(vitems) and vitems[ptr["vp"] + nv][3] == it:
+                nv += 1
+            ns = 0
+            while ptr["sp"] + ns < len(sitems) and sitems[ptr["sp"] + ns][3] == it:
+                ns += 1
+            for m in range(MACROS):
+                if max(m + 1, DAT[m]) - 2 == it:
+                    load_x(m)
             cap = JPI[it] if 0 <= it < len(JPI) else (100 if it >= len(JPI) else 0)
+            pieces = []
             while cap > 0 and jp < len(jobs):
                 kind, m = jobs[jp]
                 if kind == "x" and m > it - XLAG:
                     break
                 if kind == "x":
-                    s_x(m)
+                    pieces.extend([("x", m, q) for q in range(Q)] if XP else [("x", m, -1)])
                 else:
-                    s_l(m)
+                    pieces.extend([("l", m, q) for q in range(Q)])
                 jp += 1
                 cap -= 1
-            load_x(it - DLAG + 2)
-            while ptr["sp"] < len(sitems) and sitems[ptr["sp"]][3] == it:
-                kind, m, k, r = sitems[ptr["sp"]]
-                if kind == "z":
-                    s_zcopy(m)
-                elif kind == "p":
-                    s_plane(m, k)
-                else:
-                    s_block(m, k)
-                ptr["sp"] += 1
-                fill_s()
+            sseq = order_s(["r"] * ns, pieces)
+            vi = 0
+            nsq = len(sseq)
+            for i in range(max(nv, nsq)):
+                if i < nv:
+                    v_one()
+                if i < nsq:
+                    if sseq[i] == "r":
+                        s_one()
+                    elif sseq[i][0] == "x":
+                        s_x(sseq[i][1], sseq[i][2])
+                    else:
+                        s_l(sseq[i][1], sseq[i][2])
             if it == -4:
                 prep_w2_regroup(0)
                 prep_w2_regroup(1)
             v_regroup(it + 2)
-            v_relu(it + 2)
             if it == -3:
                 prep_w2_quant(0)
                 prep_w2_quant(1)
-            v_d(it - DLAG)
+            v_relu(it + 2)
+            for m in range(MACROS):
+                if max(m + 1, DAT[m]) == it:
+                    v_d(m)
             v_q(it + 2)
             fill_v()
             it += 1

@@ -23,26 +23,33 @@ PLANES = PASSES * PACK
 FLOPS = 2 * B * (L * H + H * D)
 
 GROUPS = [5, 6, 5]
-DAT = [m + 5 for m in range(16)]
-JPI = [1] * 2 + [2] * 11
+DAT = [m + 5 for m in range(7)] + [m + 8 for m in range(7, 16)]
+JPI = [1] * 6 + [2] * 10
 XLAG = 1
 SB = 4
 BFIRST = 1
 VORD = "bhaz"
 SMODE = "jr"
-XP = 1
-NV = 7
+XP = 2
+NV = 10
 NE = 6
 NX = 3
 ZCH = [1, 3, 4, 8]
-NVBS = [3] * 8 + [2] * 8
+NVBS = [2] * 16
 VBIAS = [0] * 8 + [1] * 8
 NH = 2
-HALF = [0] * 8 + [1] * 8
-SBK = "M" * 11 + "T" * 5
+VPL = [0] * 16
+PROD = [0] * 16
+GP = 2
+BBR = -4
+W2R = -2
+MERGE = "side"
+W2G = 0
+HALF = [0] * 10 + [1] * 6
+SBK = "M" * 9 + "T" * 7
 GFROM = 1
 SF = -9
-ZV = [0] * 8 + [1] * 8
+ZV = [0] + [1] * 15
 
 
 def tile_vae_pb_t_kernel(tc, z, x, Wd1, bd1, Wd2, bd2, out):
@@ -101,20 +108,27 @@ def tile_vae_pb_t_kernel(tc, z, x, Wd1, bd1, Wd2, bd2, out):
         bt_ps = psum_v.tile([P, P], BF16, name="psv")
         nc.tensor.transpose(bt_ps[:], b1_pad[:], ident[:])
         nc.scalar.copy(out=bst[:], in_=bt_ps[:])
-        bb = const.tile([P, PACK, P], F32, name="bb")
-        bb_ps = psum_v.tile([P, PACK, P], F32, name="psv")
-        for t in range(PACK):
-            nc.tensor.transpose(bb_ps[:, t, :], b1f[:, PACK + t:PACK + t + 1].to_broadcast([P, P]), identf[:])
-        nc.vector.tensor_copy(out=bb[:], in_=bb_ps[:])
         nc.vector.tensor_copy(out=sel[:], in_=ident[:, PACK:PLANES].unsqueeze(2).to_broadcast([P, PACK, P]))
-        nc.vector.tensor_copy(out=selh[:], in_=ident[:, PACK - NH:PACK].unsqueeze(2).to_broadcast([P, NH, W]))
         accx = const.tile([P, TILES], F32, name="accx")
         accs = const.tile([P, TILES], F32, name="accs")
         w2g = const.tile([P, PASSES, D, PACK], BF16, name="w2g", align_bytes=64)
         w2c = const.tile([P, PASSES, D], U32, name="w2c", align_bytes=64)
         w2s = const.tile([P, PASSES, D], U8, name="w2s", align_bytes=64)
 
+        bb = const.tile([P, PACK, P], F32, name="bb")
+
+        def prep_bias():
+            bb_ps = psum_v.tile([P, PACK, P], F32, name="psv")
+            for t in range(PACK):
+                nc.tensor.transpose(bb_ps[:, t, :], b1f[:, PACK + t:PACK + t + 1].to_broadcast([P, P]), identf[:])
+            nc.vector.tensor_copy(out=bb[:], in_=bb_ps[:])
+            nc.vector.tensor_copy(out=selh[:], in_=ident[:, PACK - NH:PACK].unsqueeze(2).to_broadcast([P, NH, W]))
+
         def prep_w2_regroup(c):
+            if W2G:
+                nc.gpsimd.tensor_scalar(out=w2g[:, c], in0=w2_raw[:, c].rearrange("p t n -> p n t"),
+                                        scalar1=1.0, scalar2=0.0, op0=ALU.mult, op1=ALU.add)
+                return
             nc.vector.tensor_copy(
                 out=w2g[:, c].rearrange("p (c i) t -> p c t i", i=4),
                 in_=w2_raw[:, c].rearrange("p t (c i) -> p c t i", i=4),
@@ -149,7 +163,8 @@ def tile_vae_pb_t_kernel(tc, z, x, Wd1, bd1, Wd2, bd2, out):
         def pe_plane(m, t):
             if not ok(m):
                 return
-            ps = psum_s.tile([P, W], F32, name="ps1")
+            on_v = t < VPL[m]
+            ps = (psum_v if on_v else psum_s).tile([P, W], F32, name=("psv" if on_v else "ps1"))
             nc.tensor.matmul(out=ps[:], lhsT=w1g[:, 0, t, :], rhs=st[("zT", m)][:], start=True, stop=True)
             st[("pl", m, t)] = ps
 
@@ -233,11 +248,17 @@ def tile_vae_pb_t_kernel(tc, z, x, Wd1, bd1, Wd2, bd2, out):
                 nc.scalar.activation(out=e[:].rearrange("p q d -> p (q d)"), in_=v[:].rearrange("p q d -> p (q d)"), func=ACT.Exp)
             else:
                 nc.scalar.activation(out=e[:, q, :], in_=v[:, q, :], func=ACT.Exp)
+            if (q < 0 or q == Q - 1) and PROD[m]:
+                xdone.append(m)
 
         def s_l(m, q):
             e = st[("e", m)]
             i = m * Q + q
-            nc.scalar.activation(out=e[:, q, :], in_=e[:, q, :], func=ACT.Ln, bias=ones[:], scale=1.0,
+            if m in xdone:
+                xdone.remove(m)
+                g_prod(m)
+            n = D // 2 if q < PROD[m] else D
+            nc.scalar.activation(out=e[:, q, 0:n], in_=e[:, q, 0:n], func=ACT.Ln, bias=ones[:], scale=1.0,
                                  accum_out=accs[:, i:i + 1])
 
         def order_s(rd, jb):
@@ -263,6 +284,15 @@ def tile_vae_pb_t_kernel(tc, z, x, Wd1, bd1, Wd2, bd2, out):
             if m >= GFROM:
                 nc.gpsimd.tensor_scalar(out=g0[:], in0=st[("hd0", m)][:].rearrange("p t w -> p w t"),
                                         scalar1=1.0, scalar2=0.0, op0=ALU.mult, op1=ALU.add)
+
+        def g_prod(m):
+            e = st[("e", m)]
+            q0 = 0
+            while q0 < PROD[m]:
+                n = min(GP, PROD[m] - q0)
+                nc.gpsimd.tensor_tensor(out=e[:, q0:q0 + n, 0:D // 2], in0=e[:, q0:q0 + n, 0:D // 2],
+                                        in1=e[:, q0:q0 + n, D // 2:D], op=ALU.mult)
+                q0 += n
 
         def v_regroup(m):
             if not ok(m) or m >= GFROM:
@@ -331,6 +361,10 @@ def tile_vae_pb_t_kernel(tc, z, x, Wd1, bd1, Wd2, bd2, out):
             nc.sync.dma_start(out=xt[:], in_=x_v[:, m * Q:(m + 1) * Q, :])
             st[("x", m)] = xt
 
+        if W2G:
+            prep_w2_regroup(0)
+            prep_w2_regroup(1)
+        xdone = []
         jobs = []
         m0 = 0
         for n in GROUPS:
@@ -344,13 +378,14 @@ def tile_vae_pb_t_kernel(tc, z, x, Wd1, bd1, Wd2, bd2, out):
             if ok(r + 4) and not ZV[r + 4]:
                 sitems.append(("z", r + 4, 0, r))
             if ok(r + 3):
-                pl = [("p", r + 3, t, r) for t in range(PACK - NH if HALF[r + 3] else PACK)]
+                pl = [("p", r + 3, t, r) for t in range(VPL[r + 3], PACK - NH if HALF[r + 3] else PACK)]
                 bl = [("b", r + 3, rb, r) for rb in range(NVBS[r + 3], Q)]
                 sitems.extend(bl + pl if BFIRST and r + 3 > 0 else pl + bl)
         vitems = []
         for r in range(-4, MACROS):
             h = [("h", r + 3, 0, r)] if ok(r + 3) and HALF[r + 3] else []
             z = [("z", r + 4, 0, r)] if ok(r + 4) and ZV[r + 4] else []
+            h = [("p", r + 3, t, r) for t in range(VPL[r + 3] if ok(r + 3) else 0)] + h
             aa = [("a", r, q, r) for q in range(Q)] if ok(r) else []
             bb_ = [("b", r + 2, rb, r) for rb in range(NVBS[r + 2])] if ok(r + 2) else []
             d = {"h": h, "z": z, "a": aa, "b": bb_}
@@ -386,6 +421,8 @@ def tile_vae_pb_t_kernel(tc, z, x, Wd1, bd1, Wd2, bd2, out):
                         break
                     if kind == "h":
                         pe_half(m)
+                    elif kind == "p":
+                        pe_plane(m, k)
                     else:
                         pe_block(m, k)
                 ptr["vf"] += 1
@@ -396,6 +433,9 @@ def tile_vae_pb_t_kernel(tc, z, x, Wd1, bd1, Wd2, bd2, out):
                 v_a(m, k)
             elif kind == "h":
                 v_half(m)
+            elif kind == "p":
+                nc.vector.tensor_scalar(out=hd0_of(m)[:, k, :], in0=st[("pl", m, k)][:], scalar1=b1f[:, k:k + 1], scalar2=0.0,
+                                        op0=ALU.add, op1=ALU.max)
             elif kind == "z":
                 s_zcopy(m)
             else:
@@ -417,7 +457,11 @@ def tile_vae_pb_t_kernel(tc, z, x, Wd1, bd1, Wd2, bd2, out):
         fill_s()
         it = -4
         while it <= max(DAT) or jp < len(jobs):
+            if it == BBR:
+                prep_bias()
             g_regroup(it + 2)
+            while xdone:
+                g_prod(xdone.pop(0))
             fill_v()
             fill_s()
             nv = 0
@@ -436,7 +480,7 @@ def tile_vae_pb_t_kernel(tc, z, x, Wd1, bd1, Wd2, bd2, out):
                 if kind == "x" and m > it - XLAG:
                     break
                 if kind == "x":
-                    pieces.extend([("x", m, q) for q in range(Q)] if XP else [("x", m, -1)])
+                    pieces.extend([("x", m, q) for q in range(Q)] if XP == 1 else [("x", m, -1)] + [("n", m, 0)] * 3 if XP == 2 else [("x", m, -1)])
                 else:
                     pieces.extend([("l", m, q) for q in range(Q)])
                 jp += 1
@@ -444,21 +488,34 @@ def tile_vae_pb_t_kernel(tc, z, x, Wd1, bd1, Wd2, bd2, out):
             sseq = order_s(["r"] * ns, pieces)
             vi = 0
             nsq = len(sseq)
-            for i in range(max(nv, nsq)):
-                if i < nv:
+            order = [("v", i) for i in range(nv)] + [("s", i) for i in range(nsq)]
+            if MERGE == "side":
+                order = []
+                for i in range(max(nv, nsq)):
+                    if i < nv:
+                        order.append(("v", i))
+                    if i < nsq:
+                        order.append(("s", i))
+            for who, i in order:
+                if who == "v":
                     v_one()
-                if i < nsq:
+                else:
                     if sseq[i] == "r":
                         s_one()
+                    elif sseq[i][0] == "n":
+                        continue
                     elif sseq[i][0] == "x":
                         s_x(sseq[i][1], sseq[i][2])
                     else:
                         s_l(sseq[i][1], sseq[i][2])
-            if it == -4:
+            if it == -4 and not W2G:
                 prep_w2_regroup(0)
                 prep_w2_regroup(1)
             v_regroup(it + 2)
-            if it == -3:
+            if it == -3 and not W2G:
+                prep_w2_quant(0)
+                prep_w2_quant(1)
+            if it == W2R and W2G:
                 prep_w2_quant(0)
                 prep_w2_quant(1)
             v_relu(it + 2)

@@ -47,8 +47,9 @@ MERGE = "side"
 W2G = 0
 HALF = [0] * 10 + [1] * 6
 SBK = "M" * 9 + "T" * 7
-GFROM = 1
-SF = -9
+GFROM = 2
+WARM = 0
+GRP = 5
 ZV = [0] + [1] * 15
 
 
@@ -77,7 +78,7 @@ def tile_vae_pb_t_kernel(tc, z, x, Wd1, bd1, Wd2, bd2, out):
 
         w1_raw = const.tile([P, H], BF16, name="w1_raw")
         b1_pad = const.tile([P, P], BF16, name="b1_pad")
-        w2_raw = const.tile([P, PASSES, PACK, D], BF16, name="w2_raw")
+        w2_raw = work.tile([P, PASSES, PACK, D], BF16, name="e", bufs=NE, align_bytes=64)
         b2b = const.tile([P, D], BF16, name="b2b")
         nc.vector.memset(b1_pad[:], 0.0)
         load_z(0)
@@ -92,6 +93,12 @@ def tile_vae_pb_t_kernel(tc, z, x, Wd1, bd1, Wd2, bd2, out):
         load_z(2)
         load_z(3)
 
+        if WARM:
+            warm = const.tile([P, W], BF16, name="warm")
+            nc.vector.memset(warm[:], 0.0)
+            warm_ps = psum_v.tile([P, W], F32, name="psv")
+            for k in range(WARM):
+                nc.tensor.matmul(out=warm_ps[:], lhsT=warm[:, 0:P], rhs=warm[:], start=True, stop=True)
         ident = const.tile([P, P], BF16, name="ident")
         make_identity(nc, ident[:])
         ones = const.tile([P, 1], F32, name="ones")
@@ -111,7 +118,7 @@ def tile_vae_pb_t_kernel(tc, z, x, Wd1, bd1, Wd2, bd2, out):
         nc.vector.tensor_copy(out=sel[:], in_=ident[:, PACK:PLANES].unsqueeze(2).to_broadcast([P, PACK, P]))
         accx = const.tile([P, TILES], F32, name="accx")
         accs = const.tile([P, TILES], F32, name="accs")
-        w2g = const.tile([P, PASSES, D, PACK], BF16, name="w2g", align_bytes=64)
+        w2g = work.tile([P, PASSES, D, PACK], BF16, name="e", bufs=NE, align_bytes=64)
         w2c = const.tile([P, PASSES, D], U32, name="w2c", align_bytes=64)
         w2s = const.tile([P, PASSES, D], U8, name="w2s", align_bytes=64)
 
@@ -168,24 +175,35 @@ def tile_vae_pb_t_kernel(tc, z, x, Wd1, bd1, Wd2, bd2, out):
             nc.tensor.matmul(out=ps[:], lhsT=w1g[:, 0, t, :], rhs=st[("zT", m)][:], start=True, stop=True)
             st[("pl", m, t)] = ps
 
-        def pe_block(m, rb):
-            if not ok(m):
-                return
+        def by_transposes(item):
+            kind, m, rb, r = item
+            if kind != "b":
+                return kind == "z"
+            return SBK[m] == "T" if rb >= NVBS[m] else VBIAS[m] == 1
+
+        def pe_bias(m, rb):
             on_s = rb >= NVBS[m]
             pool = psum_s if on_s else psum_v
             ps = pool.tile([P, PACK, P], F32, name=("ps1" if on_s else "psv"))
+            st[("bl", m, rb)] = ps
+            for t in range(PACK):
+                nc.tensor.matmul(out=ps[:, t, :], lhsT=bb[:, t, :], rhs=identf[:], is_transpose=True,
+                                 start=(t == 0), stop=False)
+
+        def pe_block(m, rb, biased=False):
             zT = st[("zT", m)]
-            biased = on_s or VBIAS[m]
-            if on_s and SBK[m] == "M":
-                nc.tensor.matmul(out=ps[:].rearrange("p t r -> p (t r)"), lhsT=bst[:], rhs=sel[:].rearrange("p t r -> p (t r)"), start=True, stop=False)
-            elif biased:
-                for t in range(PACK):
-                    nc.tensor.matmul(out=ps[:, t, :], lhsT=bb[:, t, :], rhs=identf[:], is_transpose=True,
-                                     start=(t == 0), stop=False)
+            if not biased:
+                on_s = rb >= NVBS[m]
+                pool = psum_s if on_s else psum_v
+                ps = pool.tile([P, PACK, P], F32, name=("ps1" if on_s else "psv"))
+                st[("bl", m, rb)] = ps
+                if on_s:
+                    nc.tensor.matmul(out=ps[:].rearrange("p t r -> p (t r)"), lhsT=bst[:], rhs=sel[:].rearrange("p t r -> p (t r)"), start=True, stop=False)
+                    biased = True
+            ps = st[("bl", m, rb)]
             for t in range(PACK):
                 nc.tensor.matmul(out=ps[:, t, :], lhsT=w1g[:, 1, t, :], rhs=zT[:, rb * P:(rb + 1) * P],
                                  start=(not biased), stop=(not biased or t == PACK - 1))
-            st[("bl", m, rb)] = ps
 
         def pe_half(m):
             ps = psum_v.tile([P, NH, W], BF16, name="psv")
@@ -242,7 +260,7 @@ def tile_vae_pb_t_kernel(tc, z, x, Wd1, bd1, Wd2, bd2, out):
         def s_x(m, q):
             v = st[("v", m)]
             if q <= 0:
-                st[("e", m)] = work.tile([P, Q, D], F32, name="e", bufs=NE)
+                st[("e", m)] = work.tile([P, Q, D], F32, name="e", bufs=NE, align_bytes=64)
             e = st[("e", m)]
             if q < 0:
                 nc.scalar.activation(out=e[:].rearrange("p q d -> p (q d)"), in_=v[:].rearrange("p q d -> p (q d)"), func=ACT.Exp)
@@ -394,38 +412,47 @@ def tile_vae_pb_t_kernel(tc, z, x, Wd1, bd1, Wd2, bd2, out):
 
         ptr = {"sp": 0, "sf": 0, "vp": 0, "vf": 0}
 
-        def fill_s():
-            while ptr["sf"] < len(sitems) and ptr["sf"] < ptr["sp"] + SB:
-                kind, m, k, r = sitems[ptr["sf"]]
-                if kind != "z" and ("zT", m) not in st:
-                    break
-                if kind == "z":
-                    pe_t(m, 0)
-                elif kind == "p":
-                    pe_plane(m, k)
-                else:
-                    pe_block(m, k)
-                ptr["sf"] += 1
+        def unit(items, i):
+            n = 1
+            if by_transposes(items[i]):
+                while GRP <= items[i][3] and i + n < len(items) and n < 4 and by_transposes(items[i + n]) and items[i + n][3] == items[i][3]:
+                    n += 1
+            return items[i:i + n]
 
-        def fill_v():
-            while ptr["vf"] < len(vitems) and ptr["vf"] < ptr["vp"] + 8 - SB:
-                kind, m, k, r = vitems[ptr["vf"]]
-                if kind == "z":
-                    pe_t(m, 1)
-                elif kind == "a":
-                    if ("cs", m) not in st:
-                        break
-                    pe_mx(m, k)
-                else:
-                    if ("zT", m) not in st:
-                        break
-                    if kind == "h":
-                        pe_half(m)
+        def fill(items, p, f, ring, on_v):
+            while ptr[f] < len(items):
+                run = unit(items, ptr[f])
+                if ptr[f] + len(run) > ptr[p] + ring:
+                    break
+                ready = True
+                for kind, m, k, r in run:
+                    if kind == "a" and ("cs", m) not in st or kind in ("p", "b", "h") and ("zT", m) not in st:
+                        ready = False
+                if not ready:
+                    break
+                tr = by_transposes(run[0])
+                if tr:
+                    for kind, m, k, r in run:
+                        if kind == "z":
+                            pe_t(m, on_v)
+                        else:
+                            pe_bias(m, k)
+                for kind, m, k, r in run:
+                    if kind == "b":
+                        pe_block(m, k, tr)
                     elif kind == "p":
                         pe_plane(m, k)
-                    else:
-                        pe_block(m, k)
-                ptr["vf"] += 1
+                    elif kind == "h":
+                        pe_half(m)
+                    elif kind == "a":
+                        pe_mx(m, k)
+                ptr[f] += len(run)
+
+        def fill_s():
+            fill(sitems, "sp", "sf", SB, 0)
+
+        def fill_v():
+            fill(vitems, "vp", "vf", 8 - SB, 1)
 
         def v_one():
             kind, m, k, r = vitems[ptr["vp"]]

@@ -35,7 +35,7 @@ NV = 10
 NE = 6
 NX = 3
 ZCH = [1, 3, 4, 8]
-NVBS = [2] * 16
+NVBS = [2] * 9 + [1] + [2] * 6
 VBIAS = [0] * 8 + [1] * 8
 NH = 2
 VPL = [0] * 16
@@ -45,8 +45,8 @@ BBR = -4
 W2R = -2
 MERGE = "side"
 W2G = 0
-HALF = [0] * 10 + [1] * 6
-SBK = "M" * 9 + "T" * 7
+HALF = [0] * 9 + [1] * 7
+SBK = "M" * 8 + "T" * 8
 GFROM = 2
 WARM = 0
 GRP = 5

from contextlib import ExitStack

import concourse.mybir as mybir
from concourse.masks import make_identity

F32 = mybir.dt.float32
BF16 = mybir.dt.bfloat16
U32 = mybir.dt.uint32
U8 = mybir.dt.uint8
FP8X4 = mybir.dt.float8_e4m3fn_x4
ALU = mybir.AluOpType
ACT = mybir.ActivationFunctionType

B, D, L, H = 8192, 512, 128, 1024
P = 128
PACK = 4
PASSES = H // (P * PACK)
TILES = B // P
Q = 4
MACROS = TILES // Q
W = Q * P
PLANES = PASSES * PACK
FLOPS = 2 * B * (L * H + H * D)

GROUPS = [5, 6, 5]
DAT = [m + 5 for m in range(7)] + [m + 8 for m in range(7, 16)]
JPI = [1] * 6 + [2] * 10
XLAG = 1
SB = 4
BFIRST = 1
VORD = "bhaz"
SMODE = "jr"
XP = 2
NV = 10
NE = 6
NX = 3
ZCH = [1, 3, 4, 8]
NVBS = [2] * 9 + [1] + [2] * 6
VBIAS = [0] * 8 + [1] * 8
NH = 2
VPL = [0] * 16
PROD = [0] * 16
GP = 2
BBR = -4
W2R = -2
MERGE = "side"
W2G = 0
HALF = [0] * 9 + [1] * 7
SBK = "M" * 8 + "T" * 8
GFROM = 2
WARM = 0
GRP = 5
ZV = [0] + [1] * 15


def tile_vae_pb_t_kernel(tc, z, x, Wd1, bd1, Wd2, bd2, out):
    nc = tc.nc
    z_v = z.rearrange("(p i) l -> p i l", i=TILES)
    x_v = x.rearrange("(p i) j -> p i j", i=TILES)
    out_v = out.rearrange("(p i) -> p i", i=TILES)
    with ExitStack() as ctx:
        const = ctx.enter_context(tc.tile_pool(name="const", bufs=1))
        work = ctx.enter_context(tc.tile_pool(name="work", bufs=2))
        psum_s = ctx.enter_context(tc.psum_pool(name="psum_s", bufs=SB))
        psum_v = ctx.enter_context(tc.psum_pool(name="psum_v", bufs=8 - SB))
        ctx.enter_context(tc.manual_schedule())

        zch = []
        m0 = 0
        for k, n in enumerate(ZCH):
            zt = const.tile([P, n * Q, L], BF16, name="zc%d" % k)
            zch.append((m0, n, zt))
            m0 += n

        def load_z(k):
            a, n, zt = zch[k]
            nc.sync.dma_start(out=zt[:], in_=z_v[:, a * Q:(a + n) * Q, :])

        w1_raw = const.tile([P, H], BF16, name="w1_raw")
        b1_pad = const.tile([P, P], BF16, name="b1_pad")
        w2_raw = work.tile([P, PASSES, PACK, D], BF16, name="e", bufs=NE, align_bytes=64)
        b2b = const.tile([P, D], BF16, name="b2b")
        nc.vector.memset(b1_pad[:], 0.0)
        load_z(0)
        nc.sync.dma_start(out=b1_pad[:, 0:PLANES].rearrange("p (c t) -> p c t", c=PASSES),
                          in_=bd1.rearrange("(c p t) -> p c t", c=PASSES, t=PACK))
        nc.sync.dma_start(out=w1_raw[:], in_=Wd1)
        load_z(1)
        w2_v = Wd2.rearrange("(c p t) n -> p c t n", c=PASSES, t=PACK)
        for c in range(PASSES):
            nc.sync.dma_start(out=w2_raw[:, c], in_=w2_v[:, c])
        nc.sync.dma_start(out=b2b[:], in_=bd2.partition_broadcast(P))
        load_z(2)
        load_z(3)

        if WARM:
            warm = const.tile([P, W], BF16, name="warm")
            nc.vector.memset(warm[:], 0.0)
            warm_ps = psum_v.tile([P, W], F32, name="psv")
            for k in range(WARM):
                nc.tensor.matmul(out=warm_ps[:], lhsT=warm[:, 0:P], rhs=warm[:], start=True, stop=True)
        ident = const.tile([P, P], BF16, name="ident")
        make_identity(nc, ident[:])
        ones = const.tile([P, 1], F32, name="ones")
        nc.vector.memset(ones[:], 1.0)
        identf = const.tile([P, P], F32, name="identf")
        make_identity(nc, identf[:])
        selh = const.tile([P, NH, W], BF16, name="selh")
        sel = const.tile([P, PACK, P], BF16, name="sel")
        b1f = const.tile([P, PLANES], F32, name="b1f")
        nc.vector.tensor_copy(out=b1f[:], in_=b1_pad[:, 0:PLANES])
        w1g = const.tile([P, PASSES, PACK, P], BF16, name="w1g")
        nc.vector.tensor_copy(out=w1g[:], in_=w1_raw[:].rearrange("l (c p t) -> l c t p", c=PASSES, t=PACK))
        bst = const.tile([P, P], BF16, name="bst")
        bt_ps = psum_v.tile([P, P], BF16, name="psv")
        nc.tensor.transpose(bt_ps[:], b1_pad[:], ident[:])
        nc.scalar.copy(out=bst[:], in_=bt_ps[:])
        nc.vector.tensor_copy(out=sel[:], in_=ident[:, PACK:PLANES].unsqueeze(2).to_broadcast([P, PACK, P]))
        accx = const.tile([P, TILES], F32, name="accx")
        accs = const.tile([P, TILES], F32, name="accs")
        w2g = work.tile([P, PASSES, D, PACK], BF16, name="e", bufs=NE, align_bytes=64)
        w2c = const.tile([P, PASSES, D], U32, name="w2c", align_bytes=64)
        w2s = const.tile([P, PASSES, D], U8, name="w2s", align_bytes=64)

        bb = const.tile([P, PACK, P], F32, name="bb")

        def prep_bias():
            bb_ps = psum_v.tile([P, PACK, P], F32, name="psv")
            for t in range(PACK):
                nc.tensor.transpose(bb_ps[:, t, :], b1f[:, PACK + t:PACK + t + 1].to_broadcast([P, P]), identf[:])
            nc.vector.tensor_copy(out=bb[:], in_=bb_ps[:])
            nc.vector.tensor_copy(out=selh[:], in_=ident[:, PACK - NH:PACK].unsqueeze(2).to_broadcast([P, NH, W]))

        def prep_w2_regroup(c):
            if W2G:
                nc.gpsimd.tensor_scalar(out=w2g[:, c], in0=w2_raw[:, c].rearrange("p t n -> p n t"),
                                        scalar1=1.0, scalar2=0.0, op0=ALU.mult, op1=ALU.add)
                return
            nc.vector.tensor_copy(
                out=w2g[:, c].rearrange("p (c i) t -> p c t i", i=4),
                in_=w2_raw[:, c].rearrange("p t (c i) -> p c t i", i=4),
            )

        def prep_w2_quant(c):
            nc.vector.quantize_mx(
                out=w2c[:, c, :].bitcast(FP8X4), scales=w2s[:, c, :],
                in_=w2g[:, c].rearrange("p n t -> p (n t)"),
            )

        st = {}

        def ok(m):
            return 0 <= m < MACROS

        def z_tile(i):
            m = i // Q
            for a, n, zt in zch:
                if a <= m < a + n:
                    return zt[:, i - a * Q, :]
            return None

        def pe_t(m, on_v):
            if not ok(m):
                return
            zt_ps = (psum_v if on_v else psum_s).tile([P, W], BF16, name=("psv" if on_v else "ps1"))
            for q in range(Q):
                nc.tensor.transpose(zt_ps[:, q * P:(q + 1) * P], z_tile(m * Q + q), ident[:])
            st[("zt_ps", m)] = zt_ps

        def pe_plane(m, t):
            if not ok(m):
                return
            on_v = t < VPL[m]
            ps = (psum_v if on_v else psum_s).tile([P, W], F32, name=("psv" if on_v else "ps1"))
            nc.tensor.matmul(out=ps[:], lhsT=w1g[:, 0, t, :], rhs=st[("zT", m)][:], start=True, stop=True)
            st[("pl", m, t)] = ps

        def by_transposes(item):
            kind, m, rb, r = item
            if kind != "b":
                return kind == "z"
            return SBK[m] == "T" if rb >= NVBS[m] else VBIAS[m] == 1

        def pe_bias(m, rb):
            on_s = rb >= NVBS[m]
            pool = psum_s if on_s else psum_v
            ps = pool.tile([P, PACK, P], F32, name=("ps1" if on_s else "psv"))
            st[("bl", m, rb)] = ps
            for t in range(PACK):
                nc.tensor.matmul(out=ps[:, t, :], lhsT=bb[:, t, :], rhs=identf[:], is_transpose=True,
                                 start=(t == 0), stop=False)

        def pe_block(m, rb, biased=False):
            zT = st[("zT", m)]
            if not biased:
                on_s = rb >= NVBS[m]
                pool = psum_s if on_s else psum_v
                ps = pool.tile([P, PACK, P], F32, name=("ps1" if on_s else "psv"))
                st[("bl", m, rb)] = ps
                if on_s:
                    nc.tensor.matmul(out=ps[:].rearrange("p t r -> p (t r)"), lhsT=bst[:], rhs=sel[:].rearrange("p t r -> p (t r)"), start=True, stop=False)
                    biased = True
            ps = st[("bl", m, rb)]
            for t in range(PACK):
                nc.tensor.matmul(out=ps[:, t, :], lhsT=w1g[:, 1, t, :], rhs=zT[:, rb * P:(rb + 1) * P],
                                 start=(not biased), stop=(not biased or t == PACK - 1))

        def pe_half(m):
            ps = psum_v.tile([P, NH, W], BF16, name="psv")
            for j in range(NH):
                nc.tensor.matmul(out=ps[:, j, :], lhsT=bst[:], rhs=selh[:, j, :], start=True, stop=False)
                nc.tensor.matmul(out=ps[:, j, :], lhsT=w1g[:, 0, PACK - NH + j, :], rhs=st[("zT", m)][:], start=False, stop=True)
            st[("hf", m)] = ps

        def pe_mx(m, q):
            cs = st[("cs", m)]
            ps = psum_v.tile([P, D], F32, name="psv")
            for c in range(PASSES):
                codes, sc = cs[c]
                nc.tensor.matmul_mx(
                    out=ps[:],
                    lhsT=codes[:, q * P:(q + 1) * P].bitcast(FP8X4), lhsT_scale=sc[:, q * P:(q + 1) * P],
                    rhs=w2c[:, c, :].bitcast(FP8X4), rhs_scale=w2s[:, c, :],
                    start=(c == 0), stop=(c == PASSES - 1),
                )
            st[("ps2", m, q)] = ps

        def s_zcopy(m):
            if not ok(m):
                return
            zT = work.tile([P, W], BF16, name="zT", bufs=4)
            if ZV[m]:
                nc.vector.tensor_copy(out=zT[:], in_=st[("zt_ps", m)][:])
            else:
                nc.scalar.copy(out=zT[:], in_=st[("zt_ps", m)][:])
            st[("zT", m)] = zT

        def hd0_of(m):
            if ("hd0", m) not in st:
                st[("hd0", m)] = work.tile([P, PACK, W], BF16, name="hd0")
            return st[("hd0", m)]

        def s_plane(m, t):
            if not ok(m):
                return
            nc.scalar.activation(out=hd0_of(m)[:, t, :], in_=st[("pl", m, t)][:], func=ACT.Relu,
                                 bias=b1f[:, t:t + 1], scale=1.0)

        def g1_of(m):
            if ("g1", m) not in st:
                st[("g1", m)] = work.tile([P, W, PACK], BF16, name="g1", bufs=3, align_bytes=64)
            return st[("g1", m)]

        def s_block(m, rb):
            if not ok(m):
                return
            nc.scalar.activation(out=g1_of(m)[:, rb * P:(rb + 1) * P, :],
                                 in_=st[("bl", m, rb)][:].rearrange("p t r -> p r t"), func=ACT.Relu)

        def s_x(m, q):
            v = st[("v", m)]
            if q <= 0:
                st[("e", m)] = work.tile([P, Q, D], F32, name="e", bufs=NE, align_bytes=64)
            e = st[("e", m)]
            if q < 0:
                nc.scalar.activation(out=e[:].rearrange("p q d -> p (q d)"), in_=v[:].rearrange("p q d -> p (q d)"), func=ACT.Exp)
            else:
                nc.scalar.activation(out=e[:, q, :], in_=v[:, q, :], func=ACT.Exp)
            if (q < 0 or q == Q - 1) and PROD[m]:
                xdone.append(m)

        def s_l(m, q):
            e = st[("e", m)]
            i = m * Q + q
            if m in xdone:
                xdone.remove(m)
                g_prod(m)
            n = D // 2 if q < PROD[m] else D
            nc.scalar.activation(out=e[:, q, 0:n], in_=e[:, q, 0:n], func=ACT.Ln, bias=ones[:], scale=1.0,
                                 accum_out=accs[:, i:i + 1])

        def order_s(rd, jb):
            if SMODE == "jr":
                return jb + rd
            if SMODE == "rj":
                return rd + jb
            seq = []
            n = len(rd)
            k = 0
            for i in range(n):
                seq.append(rd[i])
                k2 = (i + 1) * len(jb) // n
                seq.extend(jb[k:k2])
                k = k2
            return seq + jb[k:]

        def g_regroup(m):
            if not ok(m):
                return
            g0 = work.tile([P, W, PACK], BF16, name="g0", bufs=1, align_bytes=64)
            st[("g0", m)] = g0
            if m >= GFROM:
                nc.gpsimd.tensor_scalar(out=g0[:], in0=st[("hd0", m)][:].rearrange("p t w -> p w t"),
                                        scalar1=1.0, scalar2=0.0, op0=ALU.mult, op1=ALU.add)

        def g_prod(m):
            e = st[("e", m)]
            q0 = 0
            while q0 < PROD[m]:
                n = min(GP, PROD[m] - q0)
                nc.gpsimd.tensor_tensor(out=e[:, q0:q0 + n, 0:D // 2], in0=e[:, q0:q0 + n, 0:D // 2],
                                        in1=e[:, q0:q0 + n, D // 2:D], op=ALU.mult)
                q0 += n

        def v_regroup(m):
            if not ok(m) or m >= GFROM:
                return
            nc.vector.tensor_copy(
                out=st[("g0", m)][:].rearrange("p (c i) t -> p c t i", i=4),
                in_=st[("hd0", m)][:].rearrange("p t (c i) -> p c t i", i=4),
            )

        def v_block(m, rb):
            if not ok(m):
                return
            if VBIAS[m]:
                nc.vector.tensor_scalar(out=g1_of(m)[:, rb * P:(rb + 1) * P, :],
                                        in0=st[("bl", m, rb)][:].rearrange("p t r -> p r t"),
                                        scalar1=0.0, scalar2=None, op0=ALU.max)
            else:
                nc.vector.tensor_tensor(out=g1_of(m)[:, rb * P:(rb + 1) * P, :],
                                        in0=st[("bl", m, rb)][:].rearrange("p t r -> p r t"),
                                        in1=b1f[:, PACK:PLANES].unsqueeze(1).to_broadcast([P, P, PACK]), op=ALU.add)

        def v_relu(m):
            if not ok(m) or VBIAS[m] or NVBS[m] == 0:
                return
            part = g1_of(m)[:, 0:NVBS[m] * P, :]
            nc.vector.tensor_scalar(out=part, in0=part, scalar1=0.0, scalar2=None, op0=ALU.max)

        def v_half(m):
            nc.vector.tensor_scalar(out=hd0_of(m)[:, PACK - NH:PACK, :], in0=st[("hf", m)][:],
                                    scalar1=0.0, scalar2=None, op0=ALU.max)

        def v_a(m, q):
            if not ok(m):
                return
            if q == 0:
                st[("v", m)] = work.tile([P, Q, D], F32, name="v", bufs=NV)
            nc.vector.tensor_tensor(out=st[("v", m)][:, q, :], in0=st[("ps2", m, q)][:], in1=b2b[:], op=ALU.add)

        def v_d(m):
            if not ok(m):
                return
            v = st[("v", m)]
            xt = st[("x", m)]
            for q in range(Q):
                i = m * Q + q
                junkv = work.tile([P, D], BF16, name="junkv", bufs=4)
                nc.vector.scalar_tensor_tensor(out=junkv[:], in0=v[:, q, :], scalar=1.0, in1=xt[:, q, :],
                                               op0=ALU.mult, op1=ALU.mult, accum_out=accx[:, i:i + 1])

        def v_q(m):
            if not ok(m):
                return
            cs = []
            for c in range(PASSES):
                g = st[("g%d" % c, m)]
                codes = work.tile([P, W], U32, name="codes%d" % c, align_bytes=64)
                sc = work.tile([P, W], U8, name="sc%d" % c, align_bytes=64)
                nc.vector.quantize_mx(out=codes[:].bitcast(FP8X4), scales=sc[:], in_=g[:].rearrange("p w t -> p (w t)"))
                cs.append((codes, sc))
            st[("cs", m)] = cs

        def load_x(m):
            if not ok(m):
                return
            xt = work.tile([P, Q, D], BF16, name="xt", bufs=NX)
            nc.sync.dma_start(out=xt[:], in_=x_v[:, m * Q:(m + 1) * Q, :])
            st[("x", m)] = xt

        if W2G:
            prep_w2_regroup(0)
            prep_w2_regroup(1)
        xdone = []
        jobs = []
        m0 = 0
        for n in GROUPS:
            jobs.extend([("x", m) for m in range(m0, m0 + n)])
            jobs.extend([("l", m) for m in range(m0, m0 + n)])
            m0 += n
        jp = 0

        sitems = []
        for r in range(-4, MACROS):
            if ok(r + 4) and not ZV[r + 4]:
                sitems.append(("z", r + 4, 0, r))
            if ok(r + 3):
                pl = [("p", r + 3, t, r) for t in range(VPL[r + 3], PACK - NH if HALF[r + 3] else PACK)]
                bl = [("b", r + 3, rb, r) for rb in range(NVBS[r + 3], Q)]
                sitems.extend(bl + pl if BFIRST and r + 3 > 0 else pl + bl)
        vitems = []
        for r in range(-4, MACROS):
            h = [("h", r + 3, 0, r)] if ok(r + 3) and HALF[r + 3] else []
            z = [("z", r + 4, 0, r)] if ok(r + 4) and ZV[r + 4] else []
            h = [("p", r + 3, t, r) for t in range(VPL[r + 3] if ok(r + 3) else 0)] + h
            aa = [("a", r, q, r) for q in range(Q)] if ok(r) else []
            bb_ = [("b", r + 2, rb, r) for rb in range(NVBS[r + 2])] if ok(r + 2) else []
            d = {"h": h, "z": z, "a": aa, "b": bb_}
            for k in VORD:
                vitems.extend(d[k])

        ptr = {"sp": 0, "sf": 0, "vp": 0, "vf": 0}

        def unit(items, i):
            n = 1
            if by_transposes(items[i]):
                while GRP <= items[i][3] and i + n < len(items) and n < 4 and by_transposes(items[i + n]) and items[i + n][3] == items[i][3]:
                    n += 1
            return items[i:i + n]

        def fill(items, p, f, ring, on_v):
            while ptr[f] < len(items):
                run = unit(items, ptr[f])
                if ptr[f] + len(run) > ptr[p] + ring:
                    break
                ready = True
                for kind, m, k, r in run:
                    if kind == "a" and ("cs", m) not in st or kind in ("p", "b", "h") and ("zT", m) not in st:
                        ready = False
                if not ready:
                    break
                tr = by_transposes(run[0])
                if tr:
                    for kind, m, k, r in run:
                        if kind == "z":
                            pe_t(m, on_v)
                        else:
                            pe_bias(m, k)
                for kind, m, k, r in run:
                    if kind == "b":
                        pe_block(m, k, tr)
                    elif kind == "p":
                        pe_plane(m, k)
                    elif kind == "h":
                        pe_half(m)
                    elif kind == "a":
                        pe_mx(m, k)
                ptr[f] += len(run)

        def fill_s():
            fill(sitems, "sp", "sf", SB, 0)

        def fill_v():
            fill(vitems, "vp", "vf", 8 - SB, 1)

        def v_one():
            kind, m, k, r = vitems[ptr["vp"]]
            if kind == "a":
                v_a(m, k)
            elif kind == "h":
                v_half(m)
            elif kind == "p":
                nc.vector.tensor_scalar(out=hd0_of(m)[:, k, :], in0=st[("pl", m, k)][:], scalar1=b1f[:, k:k + 1], scalar2=0.0,
                                        op0=ALU.add, op1=ALU.max)
            elif kind == "z":
                s_zcopy(m)
            else:
                v_block(m, k)
            ptr["vp"] += 1
            fill_v()

        def s_one():
            kind, m, k, r = sitems[ptr["sp"]]
            if kind == "z":
                s_zcopy(m)
            elif kind == "p":
                s_plane(m, k)
            else:
                s_block(m, k)
            ptr["sp"] += 1
            fill_s()

        fill_s()
        it = -4
        while it <= max(DAT) or jp < len(jobs):
            if it == BBR:
                prep_bias()
            g_regroup(it + 2)
            while xdone:
                g_prod(xdone.pop(0))
            fill_v()
            fill_s()
            nv = 0
            while ptr["vp"] + nv < len(vitems) and vitems[ptr["vp"] + nv][3] == it:
                nv += 1
            ns = 0
            while ptr["sp"] + ns < len(sitems) and sitems[ptr["sp"] + ns][3] == it:
                ns += 1
            for m in range(MACROS):
                if max(m + 1, DAT[m]) - 2 == it:
                    load_x(m)
            cap = JPI[it] if 0 <= it < len(JPI) else (100 if it >= len(JPI) else 0)
            pieces = []
            while cap > 0 and jp < len(jobs):
                kind, m = jobs[jp]
                if kind == "x" and m > it - XLAG:
                    break
                if kind == "x":
                    pieces.extend([("x", m, q) for q in range(Q)] if XP == 1 else [("x", m, -1)] + [("n", m, 0)] * 3 if XP == 2 else [("x", m, -1)])
                else:
                    pieces.extend([("l", m, q) for q in range(Q)])
                jp += 1
                cap -= 1
            sseq = order_s(["r"] * ns, pieces)
            vi = 0
            nsq = len(sseq)
            order = [("v", i) for i in range(nv)] + [("s", i) for i in range(nsq)]
            if MERGE == "side":
                order = []
                for i in range(max(nv, nsq)):
                    if i < nv:
                        order.append(("v", i))
                    if i < nsq:
                        order.append(("s", i))
            for who, i in order:
                if who == "v":
                    v_one()
                else:
                    if sseq[i] == "r":
                        s_one()
                    elif sseq[i][0] == "n":
                        continue
                    elif sseq[i][0] == "x":
                        s_x(sseq[i][1], sseq[i][2])
                    else:
                        s_l(sseq[i][1], sseq[i][2])
            if it == -4 and not W2G:
                prep_w2_regroup(0)
                prep_w2_regroup(1)
            v_regroup(it + 2)
            if it == -3 and not W2G:
                prep_w2_quant(0)
                prep_w2_quant(1)
            if it == W2R and W2G:
                prep_w2_quant(0)
                prep_w2_quant(1)
            v_relu(it + 2)
            for m in range(MACROS):
                if max(m + 1, DAT[m]) == it:
                    v_d(m)
            v_q(it + 2)
            fill_v()
            it += 1

        res = const.tile([P, TILES], F32, name="res")
        nc.vector.tensor_sub(out=res[:], in0=accx[:], in1=accs[:])
        nc.sync.dma_start(out=out_v, in_=res[:])
